import numpy as np
import ml_dtypes


def mxq(x, axis, fmt="e4m3"):
    dtype, down = {"e4m3": (ml_dtypes.float8_e4m3fn, 7), "e5m2": (ml_dtypes.float8_e5m2, 14)}[fmt]
    v = np.moveaxis(np.asarray(x, np.float32).astype(ml_dtypes.bfloat16).astype(np.float64), axis, -1)
    blocks = v.reshape(v.shape[:-1] + (-1, 32))
    amax = np.abs(blocks).max(-1, keepdims=True)
    byte = np.maximum(np.where(amax > 0, np.frexp(amax)[1] - 1 + 127, 0) - down, 1)
    scale = np.exp2(byte - 127.0)
    codes = (blocks / scale).astype(np.float32).astype(dtype).astype(np.float64)
    return np.moveaxis((codes * scale).reshape(v.shape), -1, axis)


WIDE = False


def mx_kscale(k):
    if not WIDE:
        return np.ones(k)
    levels = np.array([10, -10, 5, -5, 0])
    a = np.random.permutation(np.resize(levels, k // 512 * 4)).reshape(k // 512, 4)
    idx = np.arange(k)
    return np.exp2(a[idx // 512, idx % 128 // 32])


BF16 = ml_dtypes.bfloat16


def bf(x):
    return np.asarray(x, np.float32).astype(BF16)


def f64(x):
    return np.asarray(x).astype(np.float64)


E2M1 = np.array([0.0, 0.5, 1.0, 1.5, 2.0, 3.0, 4.0, 6.0, -0.0, -0.5, -1.0, -1.5, -2.0, -3.0, -4.0, -6.0])


def pack_weight(w, fmt):
    k, n = w.shape
    w = f64(bf(w)).reshape(k // 32, 32, n)
    amax = np.abs(w).max(1)
    if fmt == "e4m3":
        byte = np.frexp(amax)[1] - 1 + 127 - 7
    else:
        mant, ex = np.frexp(amax / 6.0)
        byte = np.where(mant > 0.5, ex, ex - 1) + 127
    byte = np.clip(np.where(amax > 0, byte, 1), 1, 254)
    scaled = (w * np.exp2(127.0 - byte)[:, None, :]).reshape(k, n).astype(np.float32)
    by_word = np.ascontiguousarray(scaled.reshape(k // 512, 128, 4, n).transpose(0, 1, 3, 2))
    if fmt == "e4m3":
        words = by_word.astype(ml_dtypes.float8_e4m3fn).view(np.uint8)
    else:
        c = by_word.astype(ml_dtypes.float4_e2m1fn).view(np.uint8) & 0xF
        words = c[..., 0::2] | (c[..., 1::2] << 4)
    return np.ascontiguousarray(words), np.ascontiguousarray(byte.astype(np.uint8).reshape(k // 512, 16, n))


def unpack_weight(words, scales, fmt):
    g, p, n, _ = words.shape
    if fmt == "e4m3":
        vals = np.ascontiguousarray(words).view(ml_dtypes.float8_e4m3fn).astype(np.float64)
    else:
        nib = np.empty((g, p, n, 4), np.uint8)
        nib[..., 0::2] = words & 0xF
        nib[..., 1::2] = words >> 4
        vals = E2M1[nib]
    vals = vals * np.repeat(np.exp2(scales.astype(np.float64) - 127.0), 8, axis=1)[..., None]
    return vals.transpose(0, 1, 3, 2).reshape(g * 512, n)


B, Lt, La, Dt, Da, H = 2, 128, 512, 1024, 7168, 1024
F = Dt + Da


def setup_inputs():
    u = mx_kscale(F)
    scores = bf(np.random.standard_normal((B, Lt, La)) * 3.0)
    auxiliary = bf(np.random.standard_normal((B, La, Da)) * u[Dt:])
    target = bf(np.random.standard_normal((B, Lt, Dt)) * u[:Dt])
    Wf_words, Wf_scales = pack_weight(np.random.standard_normal((F, Dt)) / np.sqrt(F) / u[:, None], "e4m3")
    b_f = bf(np.random.standard_normal(Dt) * 0.1)
    return {
        "scores": scores,
        "auxiliary": auxiliary,
        "target": target,
        "Wf_words": Wf_words,
        "Wf_scales": Wf_scales,
        "b_f": b_f,
    }


def reference(scores, auxiliary, target, Wf_words, Wf_scales, b_f):
    sc = f64(scores)
    e = np.exp(sc - sc.max(-1, keepdims=True))
    attn = e / e.sum(-1, keepdims=True)
    weighted_aux = mxq(attn, 2, "e4m3") @ mxq(f64(auxiliary), 1, "e4m3")
    x = np.concatenate([f64(target), weighted_aux], axis=-1)
    y = np.tanh((mxq(x, 2, "e4m3") @ unpack_weight(Wf_words, Wf_scales, "e4m3")) + f64(b_f))
    return y.transpose(0, 2, 1)

@@ -1,0 +1,305 @@
+from contextlib import ExitStack
+
+import concourse.mybir as mybir
+from concourse.masks import make_identity
+
+BF16 = mybir.dt.bfloat16
+F32 = mybir.dt.float32
+I32 = mybir.dt.int32
+U32 = mybir.dt.uint32
+U8 = mybir.dt.uint8
+FP8X4 = mybir.dt.float8_e4m3fn_x4
+ACT = mybir.ActivationFunctionType
+
+P = 128
+PACK = 4
+K_PASS = P * PACK
+
+B, LT, LA, DT, DA = 2, 128, 512, 1024, 7168
+F = DT + DA
+GROUPS = F // K_PASS
+PAIRS = GROUPS // 2
+PAIR_W = 2 * K_PASS
+N_HALF = 512
+HALVES = DT // N_HALF
+UNITS = B * (DA // PAIR_W)
+
+VEC_M = 80
+
+RAW_BUFS = 6
+WF_LAG = 4
+
+FLOPS = 2 * B * LT * LA * DA + 2 * B * LT * F * DT
+
+
+def tile_informationfusion_pb_k_kernel(
+    tc, scores, auxiliary, target, Wf_words, Wf_scales, b_f, out
+):
+    nc = tc.nc
+    with ExitStack() as ctx:
+        ctx.enter_context(tc.manual_schedule())
+        keep = ctx.enter_context(tc.tile_pool(name="keep", bufs=1))
+        raw_pool = ctx.enter_context(tc.tile_pool(name="raw", bufs=RAW_BUFS))
+        stage = ctx.enter_context(tc.tile_pool(name="stage", bufs=3))
+        tail = ctx.enter_context(tc.tile_pool(name="tail", bufs=2))
+        psum_y = ctx.enter_context(tc.psum_pool(name="psum_y", bufs=1))
+        psum_work = ctx.enter_context(tc.psum_pool(name="psum_work", bufs=4))
+
+        wf_planes = keep.tile([P, (GROUPS // 4) * DT], U8, align_bytes=64)
+        nc.vector.memset(wf_planes[:].bitcast(I32), 0)
+        bias_row = keep.tile([P, DT], BF16)
+        nc.vector.memset(bias_row[:], 0.0)
+        ones = keep.tile([P, P], BF16)
+        nc.vector.memset(ones[:], 1.0)
+        warm = keep.tile([P, 1], F32)
+        nc.vector.memset(warm[:], 0.0)
+        nc.scalar.activation(out=warm[:], in_=warm[:], func=ACT.Exp)
+        ident_bf = keep.tile([P, P], BF16)
+        make_identity(nc, ident_bf[:])
+        ident_f32 = keep.tile([P, P], F32)
+        make_identity(nc, ident_f32[:])
+
+        sc = keep.tile([P, B, LA], BF16)
+        nc.sync.dma_start(out=sc[:], in_=scores.rearrange("b l a -> l b a"))
+        tg = keep.tile([P, B, DT], BF16)
+        nc.sync.dma_start(out=tg[:], in_=target.rearrange("b l d -> l b d"))
+        nc.sync.dma_start(out=bias_row[0:1, :], in_=b_f.rearrange("(o n) -> o n", o=1))
+
+        wf = [keep.tile([P, DT], U32, name="wf%d" % g, align_bytes=64) for g in range(GROUPS)]
+        raw = {}
+
+        def load_wf_scales():
+            for block in range(GROUPS // 4):
+                for quad in range(4):
+                    nc.sync.dma_start(
+                        out=wf_planes[
+                            32 * quad : 32 * quad + 16, block * DT : (block + 1) * DT
+                        ].bitcast(I32),
+                        in_=Wf_scales[
+                            4 * block : 4 * block + 4, 4 * quad : 4 * quad + 4, :
+                        ].bitcast(I32),
+                    )
+
+        def load_step(n):
+            g = n - WF_LAG
+            if g == 0:
+                load_wf_scales()
+            if 0 <= g < GROUPS:
+                nc.sync.dma_start(
+                    out=wf[g][:].bitcast(I32),
+                    in_=Wf_words[g].rearrange("p n t -> p (n t)").bitcast(I32),
+                )
+            if n < UNITS:
+                pair, b = n // B, n % B
+                raw_n = raw_pool.tile([P, PACK, PAIR_W], BF16, tag="raw")
+                nc.sync.dma_start(
+                    out=raw_n[:],
+                    in_=auxiliary[b, :, pair * PAIR_W : (pair + 1) * PAIR_W].rearrange(
+                        "(p j) w -> p j w", j=PACK
+                    ),
+                )
+                raw[n] = raw_n
+
+        for n in range(RAW_BUFS):
+            load_step(n)
+
+        grouped = {}
+        aux_codes = {}
+        aux_scales = {}
+        banks = {}
+        x_grouped = {}
+        x_codes = {}
+        x_scales = {}
+
+        def regroup(n):
+            grouped_n = stage.tile([P, PACK * PAIR_W], BF16, tag="grouped", align_bytes=64)
+            for gg in range(2):
+                src = raw[n][:, :, gg * K_PASS : (gg + 1) * K_PASS].rearrange(
+                    "p j (m t) -> p t m j", t=PACK
+                )
+                dst = grouped_n[:, gg * PACK * K_PASS : (gg + 1) * PACK * K_PASS].rearrange(
+                    "p (t m j) -> p t m j", t=PACK, j=PACK
+                )
+                nc.vector.tensor_copy(out=dst[:, :, 0:VEC_M, :], in_=src[:, :, 0:VEC_M, :])
+                nc.scalar.copy(out=dst[:, :, VEC_M:P, :], in_=src[:, :, VEC_M:P, :])
+            grouped[n] = grouped_n
+            load_step(n + RAW_BUFS)
+
+        def quantise_aux(n):
+            codes = stage.tile([P, PAIR_W], U32, tag="aux_codes", align_bytes=64)
+            scales = stage.tile([P, PAIR_W], U8, tag="aux_scales", align_bytes=64)
+            nc.vector.quantize_mx(out=codes[:].bitcast(FP8X4), scales=scales[:], in_=grouped[n][:])
+            aux_codes[n] = codes
+            aux_scales[n] = scales
+
+        def first_product(n):
+            b = n % B
+            banks[n] = []
+            for gg in range(2):
+                bank = psum_work.tile([P, PACK, LT], F32, tag="work")
+                for t in range(PACK):
+                    cols = slice((gg * PACK + t) * P, (gg * PACK + t + 1) * P)
+                    nc.tensor.matmul_mx(
+                        out=bank[:, t, :],
+                        lhsT=aux_codes[n][:, cols].bitcast(FP8X4),
+                        lhsT_scale=aux_scales[n][:, cols],
+                        rhs=attn_codes[:, b * LT : (b + 1) * LT].bitcast(FP8X4),
+                        rhs_scale=attn_scales[:, b * LT : (b + 1) * LT],
+                        start=True,
+                        stop=True,
+                    )
+                banks[n].append(bank)
+
+        def round_x(n):
+            x_n = stage.tile([P, 2 * PACK * LT], BF16, tag="x_grouped", align_bytes=64)
+            for gg in range(2):
+                nc.scalar.copy(
+                    out=x_n[:, gg * PACK * LT : (gg + 1) * PACK * LT].rearrange(
+                        "p (l t) -> p l t", t=PACK
+                    ),
+                    in_=banks[n][gg][:].rearrange("p t l -> p l t"),
+                )
+            x_grouped[(n // B + 1, n % B)] = x_n
+
+        def quantise_x(pair, b):
+            codes = keep.tile([P, 2 * LT], U32, name="x_codes_%d_%d" % (pair, b), align_bytes=64)
+            scales = keep.tile([P, 2 * LT], U8, name="x_scales_%d_%d" % (pair, b), align_bytes=64)
+            nc.vector.quantize_mx(
+                out=codes[:].bitcast(FP8X4), scales=scales[:], in_=x_grouped[(pair, b)][:]
+            )
+            x_codes[(pair, b)] = codes
+            x_scales[(pair, b)] = scales
+
+        y = {}
+        for b in range(B):
+            for h in range(HALVES):
+                y[(b, h)] = psum_y.tile([P, N_HALF], F32, name="y_%d_%d" % (b, h))
+
+        def second_product(pair):
+            for gg in range(2):
+                g = 2 * pair + gg
+                first_row = 4 * (g % 4)
+                for b in range(B):
+                    for h in range(HALVES):
+                        plane_col = (g // 4) * DT + h * N_HALF
+                        nc.tensor.matmul_mx(
+                            out=y[(b, h)][:],
+                            lhsT=x_codes[(pair, b)][:, gg * LT : (gg + 1) * LT].bitcast(FP8X4),
+                            lhsT_scale=x_scales[(pair, b)][:, gg * LT : (gg + 1) * LT],
+                            rhs=wf[g][:, h * N_HALF : (h + 1) * N_HALF].bitcast(FP8X4),
+                            rhs_scale=wf_planes[first_row:P, plane_col : plane_col + N_HALF],
+                            start=(g == 0),
+                            stop=(g == GROUPS - 1),
+                        )
+
+        row_max = keep.tile([P, B], F32)
+        nc.vector.reduce_max(out=row_max[:], in_=sc[:], axis=mybir.AxisListType.X)
+        neg_max = keep.tile([P, B], F32)
+        nc.vector.tensor_scalar_mul(out=neg_max[:], in0=row_max[:], scalar1=-1.0)
+        expo = keep.tile([P, B, LA], F32)
+        row_sum = keep.tile([P, B], F32)
+        for b in range(B):
+            nc.scalar.activation(
+                out=expo[:, b, :],
+                in_=sc[:, b, :],
+                func=ACT.Exp,
+                bias=neg_max[:, b : b + 1],
+                scale=1.0,
+                accum_out=row_sum[:, b : b + 1],
+            )
+        inv_sum = keep.tile([P, B], F32)
+        nc.vector.reciprocal(out=inv_sum[:], in_=row_sum[:])
+        attn = keep.tile([P, B, PACK, P], BF16)
+        for b in range(B):
+            nc.vector.tensor_scalar_mul(
+                out=attn[:, b, :, :],
+                in0=expo[:, b, :].rearrange("l (p j) -> l j p", j=PACK),
+                scalar1=inv_sum[:, b : b + 1],
+            )
+
+        regroup(0)
+
+        attn_grouped = keep.tile([P, B * PACK * LT], BF16, align_bytes=64)
+        for b in range(B):
+            attn_t = psum_work.tile([P, PACK, LT], BF16, tag="work")
+            for j in range(PACK):
+                nc.tensor.transpose(attn_t[:, j, :], attn[:, b, j, :], ident_bf[:])
+            nc.scalar.copy(
+                out=attn_grouped[:, b * PACK * LT : (b + 1) * PACK * LT].rearrange(
+                    "p (l j) -> p l j", j=PACK
+                ),
+                in_=attn_t[:].rearrange("p j l -> p l j"),
+            )
+        attn_codes = keep.tile([P, B * LT], U32, align_bytes=64)
+        attn_scales = keep.tile([P, B * LT], U8, align_bytes=64)
+        nc.vector.quantize_mx(
+            out=attn_codes[:].bitcast(FP8X4), scales=attn_scales[:], in_=attn_grouped[:]
+        )
+
+        tg_words = tg[:].bitcast(F32)
+        for b in range(B):
+            tg_t = psum_work.tile([P, 2, 2, LT], F32, tag="work")
+            for gg in range(2):
+                for u in range(2):
+                    first = gg * (K_PASS // 2) + u
+                    nc.tensor.transpose(
+                        tg_t[:, gg, u, :],
+                        tg_words[:, b, first : (gg + 1) * (K_PASS // 2) : 2],
+                        ident_f32[:],
+                    )
+            x_n = stage.tile([P, 2 * PACK * LT], BF16, tag="x_grouped", align_bytes=64)
+            nc.scalar.copy(
+                out=x_n[:].bitcast(F32).rearrange("p (g l u) -> p g l u", g=2, u=2),
+                in_=tg_t[:].rearrange("p g u l -> p g l u"),
+            )
+            x_grouped[(0, b)] = x_n
+
+        bias = keep.tile([P, HALVES, PACK, P], F32)
+        for h in range(HALVES):
+            bias_ps = psum_work.tile([P, N_HALF], F32, tag="work")
+            nc.tensor.matmul(
+                out=bias_ps[:],
+                lhsT=ones[:],
+                rhs=bias_row[:, h * N_HALF : (h + 1) * N_HALF],
+                start=True,
+                stop=True,
+            )
+            nc.vector.tensor_copy(
+                out=bias[:, h, :, :], in_=bias_ps[:].rearrange("l (n c) -> l c n", c=PACK)
+            )
+        for b in range(B):
+            quantise_x(0, b)
+
+        for n in range(UNITS + WF_LAG + 2):
+            if n + 1 < UNITS:
+                regroup(n + 1)
+            if n < UNITS:
+                quantise_aux(n)
+                first_product(n)
+            if 0 <= n - 1 < UNITS:
+                round_x(n - 1)
+            if 0 <= n - 2 < UNITS:
+                quantise_x((n - 2) // B + 1, (n - 2) % B)
+            if n >= WF_LAG + 1 and (n - WF_LAG - 1) % 2 == 0:
+                second_product((n - WF_LAG - 1) // 2)
+
+        for b in range(B):
+            for h in range(HALVES):
+                y_sb = tail.tile([P, PACK, P], F32, tag="y_sb")
+                nc.vector.tensor_tensor(
+                    out=y_sb[:],
+                    in0=y[(b, h)][:].rearrange("l (n c) -> l c n", c=PACK),
+                    in1=bias[:, h, :, :],
+                    op=mybir.AluOpType.add,
+                )
+                y_t = psum_work.tile([P, PACK, LT], F32, tag="work")
+                for c in range(PACK):
+                    nc.tensor.transpose(y_t[:, c, :], y_sb[:, c, :], ident_f32[:])
+                o_sb = tail.tile([P, PACK, LT], F32, tag="o_sb")
+                nc.scalar.activation(out=o_sb[:], in_=y_t[:], func=ACT.Tanh)
+                nc.sync.dma_start(
+                    out=out[b, h * N_HALF : (h + 1) * N_HALF, :].rearrange(
+                        "(n c) l -> n (c l)", c=PACK
+                    ),
+                    in_=o_sb[:].rearrange("n c l -> n (c l)"),
+                )

@@ -115,13 +115,13 @@ def tile_informationfusion_pb_k_kernel(
             grouped_n = stage.tile([P, PACK * PAIR_W], BF16, tag="grouped", align_bytes=64)
             for gg in range(2):
                 src = raw[n][:, :, gg * K_PASS : (gg + 1) * K_PASS].rearrange(
-                    "p j (m t) -> p t m j", t=PACK
+                    "p j (m t) -> p m j t", t=PACK
                 )
                 dst = grouped_n[:, gg * PACK * K_PASS : (gg + 1) * PACK * K_PASS].rearrange(
-                    "p (t m j) -> p t m j", t=PACK, j=PACK
+                    "p (t m j) -> p m j t", t=PACK, j=PACK
                 )
-                nc.vector.tensor_copy(out=dst[:, :, 0:VEC_M, :], in_=src[:, :, 0:VEC_M, :])
-                nc.scalar.copy(out=dst[:, :, VEC_M:P, :], in_=src[:, :, VEC_M:P, :])
+                nc.vector.tensor_copy(out=dst[:, 0:VEC_M, :, :], in_=src[:, 0:VEC_M, :, :])
+                nc.scalar.copy(out=dst[:, VEC_M:P, :, :], in_=src[:, VEC_M:P, :, :])
             grouped[n] = grouped_n
             load_step(n + RAW_BUFS)
 

@@ -18,16 +18,17 @@ K_PASS = P * PACK
 B, LT, LA, DT, DA = 2, 128, 512, 1024, 7168
 F = DT + DA
 GROUPS = F // K_PASS
-PAIRS = GROUPS // 2
-PAIR_W = 2 * K_PASS
+TARGET_GROUPS = DT // K_PASS
+AUX_GROUPS = DA // K_PASS
 N_HALF = 512
 HALVES = DT // N_HALF
-UNITS = B * (DA // PAIR_W)
+
+LOAD_GROUPS = 4
+RAW_BUFS = 4
+WF_FIRST_LOAD = 3
+WF_PER_LOAD = 2
 
 VEC_M = 80
-
-RAW_BUFS = 6
-WF_LAG = 4
 
 FLOPS = 2 * B * LT * LA * DA + 2 * B * LT * F * DT
 
@@ -36,6 +37,19 @@ def tile_informationfusion_pb_k_kernel(
     tc, scores, auxiliary, target, Wf_words, Wf_scales, b_f, out
 ):
     nc = tc.nc
+
+    starts = [0] + list(range(AUX_GROUPS % LOAD_GROUPS, AUX_GROUPS, LOAD_GROUPS))
+    ends = starts[1:] + [AUX_GROUPS]
+    loads = [(start, end, b) for start, end in zip(starts, ends) for b in range(B)]
+    units = []
+    first_unit = {}
+    for k, (start, end, b) in enumerate(loads):
+        first_unit[k] = len(units)
+        for a in range(start, end):
+            units.append((k, a - start, b, TARGET_GROUPS + a))
+    last_load = len(loads) - 1
+    trailing_group = WF_PER_LOAD * (last_load - WF_FIRST_LOAD)
+
     with ExitStack() as ctx:
         ctx.enter_context(tc.manual_schedule())
         keep = ctx.enter_context(tc.tile_pool(name="keep", bufs=1))
@@ -68,40 +82,39 @@ def tile_informationfusion_pb_k_kernel(
         wf = [keep.tile([P, DT], U32, name="wf%d" % g, align_bytes=64) for g in range(GROUPS)]
         raw = {}
 
-        def load_wf_scales():
-            for block in range(GROUPS // 4):
-                for quad in range(4):
-                    nc.sync.dma_start(
-                        out=wf_planes[
-                            32 * quad : 32 * quad + 16, block * DT : (block + 1) * DT
-                        ].bitcast(I32),
-                        in_=Wf_scales[
-                            4 * block : 4 * block + 4, 4 * quad : 4 * quad + 4, :
-                        ].bitcast(I32),
-                    )
+        def load_wf(g):
+            nc.sync.dma_start(
+                out=wf[g][:].bitcast(I32),
+                in_=Wf_words[g].rearrange("p n t -> p (n t)").bitcast(I32),
+            )
 
-        def load_step(n):
-            g = n - WF_LAG
-            if g == 0:
-                load_wf_scales()
-            if 0 <= g < GROUPS:
-                nc.sync.dma_start(
-                    out=wf[g][:].bitcast(I32),
-                    in_=Wf_words[g].rearrange("p n t -> p (n t)").bitcast(I32),
-                )
-            if n < UNITS:
-                pair, b = n // B, n % B
-                raw_n = raw_pool.tile([P, PACK, PAIR_W], BF16, tag="raw")
-                nc.sync.dma_start(
-                    out=raw_n[:],
-                    in_=auxiliary[b, :, pair * PAIR_W : (pair + 1) * PAIR_W].rearrange(
-                        "(p j) w -> p j w", j=PACK
-                    ),
-                )
-                raw[n] = raw_n
+        def load_wf_scales(block, quad):
+            nc.sync.dma_start(
+                out=wf_planes[32 * quad : 32 * quad + 16, block * DT : (block + 1) * DT].bitcast(I32),
+                in_=Wf_scales[4 * block : 4 * block + 4, 4 * quad : 4 * quad + 4, :].bitcast(I32),
+            )
 
-        for n in range(RAW_BUFS):
-            load_step(n)
+        def load_aux(k):
+            if WF_FIRST_LOAD <= k < last_load:
+                for g in range(WF_PER_LOAD * (k - WF_FIRST_LOAD), WF_PER_LOAD * (k - WF_FIRST_LOAD + 1)):
+                    load_wf(g)
+            start, end, b = loads[k]
+            raw_k = raw_pool.tile([P, PACK, (end - start) * K_PASS], BF16, tag="raw")
+            nc.sync.dma_start(
+                out=raw_k[:],
+                in_=auxiliary[b, :, start * K_PASS : end * K_PASS].rearrange(
+                    "(p j) w -> p j w", j=PACK
+                ),
+            )
+            raw[k] = raw_k
+            for s in (2 * k, 2 * k + 1):
+                load_wf_scales(s // 4, s % 4)
+            if k == last_load:
+                for g in range(trailing_group, GROUPS):
+                    load_wf(g)
+
+        for k in range(RAW_BUFS):
+            load_aux(k)
 
         grouped = {}
         aux_codes = {}
@@ -111,86 +124,79 @@ def tile_informationfusion_pb_k_kernel(
         x_codes = {}
         x_scales = {}
 
-        def regroup(n):
-            grouped_n = stage.tile([P, PACK * PAIR_W], BF16, tag="grouped", align_bytes=64)
-            for gg in range(2):
-                src = raw[n][:, :, gg * K_PASS : (gg + 1) * K_PASS].rearrange(
-                    "p j (m t) -> p m j t", t=PACK
-                )
-                dst = grouped_n[:, gg * PACK * K_PASS : (gg + 1) * PACK * K_PASS].rearrange(
-                    "p (t m j) -> p m j t", t=PACK, j=PACK
-                )
-                nc.vector.tensor_copy(out=dst[:, 0:VEC_M, :, :], in_=src[:, 0:VEC_M, :, :])
-                nc.scalar.copy(out=dst[:, VEC_M:P, :, :], in_=src[:, VEC_M:P, :, :])
-            grouped[n] = grouped_n
-            load_step(n + RAW_BUFS)
-
-        def quantise_aux(n):
-            codes = stage.tile([P, PAIR_W], U32, tag="aux_codes", align_bytes=64)
-            scales = stage.tile([P, PAIR_W], U8, tag="aux_scales", align_bytes=64)
-            nc.vector.quantize_mx(out=codes[:].bitcast(FP8X4), scales=scales[:], in_=grouped[n][:])
-            aux_codes[n] = codes
-            aux_scales[n] = scales
-
-        def first_product(n):
-            b = n % B
-            banks[n] = []
-            for gg in range(2):
-                bank = psum_work.tile([P, PACK, LT], F32, tag="work")
-                for t in range(PACK):
-                    cols = slice((gg * PACK + t) * P, (gg * PACK + t + 1) * P)
-                    nc.tensor.matmul_mx(
-                        out=bank[:, t, :],
-                        lhsT=aux_codes[n][:, cols].bitcast(FP8X4),
-                        lhsT_scale=aux_scales[n][:, cols],
-                        rhs=attn_codes[:, b * LT : (b + 1) * LT].bitcast(FP8X4),
-                        rhs_scale=attn_scales[:, b * LT : (b + 1) * LT],
-                        start=True,
-                        stop=True,
-                    )
-                banks[n].append(bank)
-
-        def round_x(n):
-            x_n = stage.tile([P, 2 * PACK * LT], BF16, tag="x_grouped", align_bytes=64)
-            for gg in range(2):
-                nc.scalar.copy(
-                    out=x_n[:, gg * PACK * LT : (gg + 1) * PACK * LT].rearrange(
-                        "p (l t) -> p l t", t=PACK
-                    ),
-                    in_=banks[n][gg][:].rearrange("p t l -> p l t"),
-                )
-            x_grouped[(n // B + 1, n % B)] = x_n
-
-        def quantise_x(pair, b):
-            codes = keep.tile([P, 2 * LT], U32, name="x_codes_%d_%d" % (pair, b), align_bytes=64)
-            scales = keep.tile([P, 2 * LT], U8, name="x_scales_%d_%d" % (pair, b), align_bytes=64)
-            nc.vector.quantize_mx(
-                out=codes[:].bitcast(FP8X4), scales=scales[:], in_=x_grouped[(pair, b)][:]
+        def regroup(u):
+            k, place, b, g = units[u]
+            grouped_u = stage.tile([P, PACK * K_PASS], BF16, tag="grouped", align_bytes=64)
+            src = raw[k][:, :, place * K_PASS : (place + 1) * K_PASS].rearrange(
+                "p j (m t) -> p m j t", t=PACK
             )
-            x_codes[(pair, b)] = codes
-            x_scales[(pair, b)] = scales
+            dst = grouped_u[:].rearrange("p (t m j) -> p m j t", t=PACK, j=PACK)
+            nc.vector.tensor_copy(out=dst[:, 0:VEC_M, :, :], in_=src[:, 0:VEC_M, :, :])
+            nc.scalar.copy(out=dst[:, VEC_M:P, :, :], in_=src[:, VEC_M:P, :, :])
+            grouped[u] = grouped_u
+            if u + 1 == len(units) or units[u + 1][0] != k:
+                if k + RAW_BUFS <= last_load:
+                    load_aux(k + RAW_BUFS)
+
+        def quantise_aux(u):
+            codes = stage.tile([P, K_PASS], U32, tag="aux_codes", align_bytes=64)
+            scales = stage.tile([P, K_PASS], U8, tag="aux_scales", align_bytes=64)
+            nc.vector.quantize_mx(out=codes[:].bitcast(FP8X4), scales=scales[:], in_=grouped[u][:])
+            aux_codes[u] = codes
+            aux_scales[u] = scales
+
+        def first_product(u):
+            k, place, b, g = units[u]
+            bank = psum_work.tile([P, PACK, LT], F32, tag="work")
+            for t in range(PACK):
+                nc.tensor.matmul_mx(
+                    out=bank[:, t, :],
+                    lhsT=aux_codes[u][:, t * P : (t + 1) * P].bitcast(FP8X4),
+                    lhsT_scale=aux_scales[u][:, t * P : (t + 1) * P],
+                    rhs=attn_codes[:, b * LT : (b + 1) * LT].bitcast(FP8X4),
+                    rhs_scale=attn_scales[:, b * LT : (b + 1) * LT],
+                    start=True,
+                    stop=True,
+                )
+            banks[u] = bank
+
+        def round_x(u):
+            x_u = stage.tile([P, PACK * LT], BF16, tag="x_grouped", align_bytes=64)
+            nc.scalar.copy(
+                out=x_u[:].rearrange("p (l t) -> p l t", t=PACK),
+                in_=banks[u][:].rearrange("p t l -> p l t"),
+            )
+            x_grouped[u] = x_u
+
+        def quantise_x(u):
+            k, place, b, g = units[u]
+            codes = keep.tile([P, LT], U32, name="x_codes_%d_%d" % (g, b), align_bytes=64)
+            scales = keep.tile([P, LT], U8, name="x_scales_%d_%d" % (g, b), align_bytes=64)
+            nc.vector.quantize_mx(
+                out=codes[:].bitcast(FP8X4), scales=scales[:], in_=x_grouped[u][:]
+            )
+            x_codes[(g, b)] = codes[:]
+            x_scales[(g, b)] = scales[:]
 
         y = {}
         for b in range(B):
             for h in range(HALVES):
                 y[(b, h)] = psum_y.tile([P, N_HALF], F32, name="y_%d_%d" % (b, h))
 
-        def second_product(pair):
-            for gg in range(2):
-                g = 2 * pair + gg
-                first_row = 4 * (g % 4)
-                for b in range(B):
-                    for h in range(HALVES):
-                        plane_col = (g // 4) * DT + h * N_HALF
-                        nc.tensor.matmul_mx(
-                            out=y[(b, h)][:],
-                            lhsT=x_codes[(pair, b)][:, gg * LT : (gg + 1) * LT].bitcast(FP8X4),
-                            lhsT_scale=x_scales[(pair, b)][:, gg * LT : (gg + 1) * LT],
-                            rhs=wf[g][:, h * N_HALF : (h + 1) * N_HALF].bitcast(FP8X4),
-                            rhs_scale=wf_planes[first_row:P, plane_col : plane_col + N_HALF],
-                            start=(g == 0),
-                            stop=(g == GROUPS - 1),
-                        )
+        def second_product(g):
+            first_row = 4 * (g % 4)
+            for b in range(B):
+                for h in range(HALVES):
+                    plane_col = (g // 4) * DT + h * N_HALF
+                    nc.tensor.matmul_mx(
+                        out=y[(b, h)][:],
+                        lhsT=x_codes[(g, b)].bitcast(FP8X4),
+                        lhsT_scale=x_scales[(g, b)],
+                        rhs=wf[g][:, h * N_HALF : (h + 1) * N_HALF].bitcast(FP8X4),
+                        rhs_scale=wf_planes[first_row:P, plane_col : plane_col + N_HALF],
+                        start=(g == 0),
+                        stop=(g == GROUPS - 1),
+                    )
 
         row_max = keep.tile([P, B], F32)
         nc.vector.reduce_max(out=row_max[:], in_=sc[:], axis=mybir.AxisListType.X)
@@ -237,22 +243,24 @@ def tile_informationfusion_pb_k_kernel(
         )
 
         tg_words = tg[:].bitcast(F32)
+        tg_grouped = {}
         for b in range(B):
-            tg_t = psum_work.tile([P, 2, 2, LT], F32, tag="work")
-            for gg in range(2):
+            tg_t = psum_work.tile([P, TARGET_GROUPS, 2, LT], F32, tag="work")
+            for g in range(TARGET_GROUPS):
                 for u in range(2):
-                    first = gg * (K_PASS // 2) + u
                     nc.tensor.transpose(
-                        tg_t[:, gg, u, :],
-                        tg_words[:, b, first : (gg + 1) * (K_PASS // 2) : 2],
+                        tg_t[:, g, u, :],
+                        tg_words[:, b, g * (K_PASS // 2) + u : (g + 1) * (K_PASS // 2) : 2],
                         ident_f32[:],
                     )
-            x_n = stage.tile([P, 2 * PACK * LT], BF16, tag="x_grouped", align_bytes=64)
+            tg_b = keep.tile(
+                [P, TARGET_GROUPS * PACK * LT], BF16, name="tg_grouped_%d" % b, align_bytes=64
+            )
             nc.scalar.copy(
-                out=x_n[:].bitcast(F32).rearrange("p (g l u) -> p g l u", g=2, u=2),
+                out=tg_b[:].bitcast(F32).rearrange("p (g l u) -> p g l u", g=TARGET_GROUPS, u=2),
                 in_=tg_t[:].rearrange("p g u l -> p g l u"),
             )
-            x_grouped[(0, b)] = x_n
+            tg_grouped[b] = tg_b
 
         bias = keep.tile([P, HALVES, PACK, P], F32)
         for h in range(HALVES):
@@ -268,20 +276,32 @@ def tile_informationfusion_pb_k_kernel(
                 out=bias[:, h, :, :], in_=bias_ps[:].rearrange("l (n c) -> l c n", c=PACK)
             )
         for b in range(B):
-            quantise_x(0, b)
+            codes = keep.tile([P, TARGET_GROUPS * LT], U32, name="tg_codes_%d" % b, align_bytes=64)
+            scales = keep.tile([P, TARGET_GROUPS * LT], U8, name="tg_scales_%d" % b, align_bytes=64)
+            nc.vector.quantize_mx(
+                out=codes[:].bitcast(FP8X4), scales=scales[:], in_=tg_grouped[b][:]
+            )
+            for g in range(TARGET_GROUPS):
+                x_codes[(g, b)] = codes[:, g * LT : (g + 1) * LT]
+                x_scales[(g, b)] = scales[:, g * LT : (g + 1) * LT]
 
-        for n in range(UNITS + WF_LAG + 2):
-            if n + 1 < UNITS:
+        steady_from = first_unit[WF_FIRST_LOAD]
+        trailing_from = first_unit[last_load] - 1
+        units_per_group = LOAD_GROUPS // WF_PER_LOAD
+        for n in range(trailing_from + GROUPS - trailing_group):
+            if n + 1 < len(units):
                 regroup(n + 1)
-            if n < UNITS:
+            if n < len(units):
                 quantise_aux(n)
                 first_product(n)
-            if 0 <= n - 1 < UNITS:
+            if 0 <= n - 1 < len(units):
                 round_x(n - 1)
-            if 0 <= n - 2 < UNITS:
-                quantise_x((n - 2) // B + 1, (n - 2) % B)
-            if n >= WF_LAG + 1 and (n - WF_LAG - 1) % 2 == 0:
-                second_product((n - WF_LAG - 1) // 2)
+            if 0 <= n - 2 < len(units):
+                quantise_x(n - 2)
+            if n >= trailing_from:
+                second_product(trailing_group + n - trailing_from)
+            elif n >= steady_from and (n - steady_from) % units_per_group == 0:
+                second_product((n - steady_from) // units_per_group)
 
         for b in range(B):
             for h in range(HALVES):

@@ -25,10 +25,10 @@ HALVES = DT // N_HALF
 
 LOAD_GROUPS = 4
 RAW_BUFS = 4
-WF_FIRST_LOAD = 3
-WF_PER_LOAD = 2
+SP_FIRST = 14
+TARGET_STEP = 4
 
-VEC_M = 80
+VEC_M = 76
 
 FLOPS = 2 * B * LT * LA * DA + 2 * B * LT * F * DT
 
@@ -48,7 +48,6 @@ def tile_informationfusion_pb_k_kernel(
         for a in range(start, end):
             units.append((k, a - start, b, TARGET_GROUPS + a))
     last_load = len(loads) - 1
-    trailing_group = WF_PER_LOAD * (last_load - WF_FIRST_LOAD)
 
     with ExitStack() as ctx:
         ctx.enter_context(tc.manual_schedule())
@@ -76,13 +75,13 @@ def tile_informationfusion_pb_k_kernel(
         sc = keep.tile([P, B, LA], BF16)
         nc.sync.dma_start(out=sc[:], in_=scores.rearrange("b l a -> l b a"))
         tg = keep.tile([P, B, DT], BF16)
-        nc.sync.dma_start(out=tg[:], in_=target.rearrange("b l d -> l b d"))
-        nc.sync.dma_start(out=bias_row[0:1, :], in_=b_f.rearrange("(o n) -> o n", o=1))
 
         wf = [keep.tile([P, DT], U32, name="wf%d" % g, align_bytes=64) for g in range(GROUPS)]
+        wf_queued = set()
         raw = {}
 
         def load_wf(g):
+            wf_queued.add(g)
             nc.sync.dma_start(
                 out=wf[g][:].bitcast(I32),
                 in_=Wf_words[g].rearrange("p n t -> p (n t)").bitcast(I32),
@@ -95,8 +94,8 @@ def tile_informationfusion_pb_k_kernel(
             )
 
         def load_aux(k):
-            if WF_FIRST_LOAD <= k < last_load:
-                for g in range(WF_PER_LOAD * (k - WF_FIRST_LOAD), WF_PER_LOAD * (k - WF_FIRST_LOAD + 1)):
+            for g in range(GROUPS):
+                if g not in wf_queued and SP_FIRST + g < first_unit[k] - 2:
                     load_wf(g)
             start, end, b = loads[k]
             raw_k = raw_pool.tile([P, PACK, (end - start) * K_PASS], BF16, tag="raw")
@@ -107,11 +106,16 @@ def tile_informationfusion_pb_k_kernel(
                 ),
             )
             raw[k] = raw_k
-            for s in (2 * k, 2 * k + 1):
-                load_wf_scales(s // 4, s % 4)
+            if k < GROUPS // 4:
+                for quad in range(4):
+                    load_wf_scales(k, quad)
+            if k == B - 1:
+                nc.sync.dma_start(out=tg[:], in_=target.rearrange("b l d -> l b d"))
+                nc.sync.dma_start(out=bias_row[0:1, :], in_=b_f.rearrange("(o n) -> o n", o=1))
             if k == last_load:
-                for g in range(trailing_group, GROUPS):
-                    load_wf(g)
+                for g in range(GROUPS):
+                    if g not in wf_queued:
+                        load_wf(g)
 
         for k in range(RAW_BUFS):
             load_aux(k)
@@ -183,20 +187,39 @@ def tile_informationfusion_pb_k_kernel(
             for h in range(HALVES):
                 y[(b, h)] = psum_y.tile([P, N_HALF], F32, name="y_%d_%d" % (b, h))
 
-        def second_product(g):
+        def second_product(g, b):
             first_row = 4 * (g % 4)
-            for b in range(B):
-                for h in range(HALVES):
-                    plane_col = (g // 4) * DT + h * N_HALF
-                    nc.tensor.matmul_mx(
-                        out=y[(b, h)][:],
-                        lhsT=x_codes[(g, b)].bitcast(FP8X4),
-                        lhsT_scale=x_scales[(g, b)],
-                        rhs=wf[g][:, h * N_HALF : (h + 1) * N_HALF].bitcast(FP8X4),
-                        rhs_scale=wf_planes[first_row:P, plane_col : plane_col + N_HALF],
-                        start=(g == 0),
-                        stop=(g == GROUPS - 1),
-                    )
+            for h in range(HALVES):
+                plane_col = (g // 4) * DT + h * N_HALF
+                nc.tensor.matmul_mx(
+                    out=y[(b, h)][:],
+                    lhsT=x_codes[(g, b)].bitcast(FP8X4),
+                    lhsT_scale=x_scales[(g, b)],
+                    rhs=wf[g][:, h * N_HALF : (h + 1) * N_HALF].bitcast(FP8X4),
+                    rhs_scale=wf_planes[first_row:P, plane_col : plane_col + N_HALF],
+                    start=(g == 0),
+                    stop=(g == GROUPS - 1),
+                )
+
+        x_step = {}
+        for u, (k, place, b, g) in enumerate(units):
+            x_step[(g, b)] = u + 3
+
+        def step(n):
+            if n + 1 < len(units):
+                regroup(n + 1)
+            if n < len(units):
+                quantise_aux(n)
+            if 0 <= n - 1 < len(units):
+                first_product(n - 1)
+            if 0 <= n - 2 < len(units):
+                round_x(n - 2)
+            if 0 <= n - 3 < len(units):
+                quantise_x(n - 3)
+            for g in range(GROUPS):
+                for b in range(B):
+                    if max(SP_FIRST + g, x_step.get((g, b), 0)) == n:
+                        second_product(g, b)
 
         row_max = keep.tile([P, B], F32)
         nc.vector.reduce_max(out=row_max[:], in_=sc[:], axis=mybir.AxisListType.X)
@@ -213,6 +236,7 @@ def tile_informationfusion_pb_k_kernel(
                 scale=1.0,
                 accum_out=row_sum[:, b : b + 1],
             )
+        regroup(0)
         inv_sum = keep.tile([P, B], F32)
         nc.vector.reciprocal(out=inv_sum[:], in_=row_sum[:])
         attn = keep.tile([P, B, PACK, P], BF16)
@@ -222,9 +246,7 @@ def tile_informationfusion_pb_k_kernel(
                 in0=expo[:, b, :].rearrange("l (p j) -> l j p", j=PACK),
                 scalar1=inv_sum[:, b : b + 1],
             )
-
-        regroup(0)
-
+        step(0)
         attn_grouped = keep.tile([P, B * PACK * LT], BF16, align_bytes=64)
         for b in range(B):
             attn_t = psum_work.tile([P, PACK, LT], BF16, tag="work")
@@ -241,40 +263,45 @@ def tile_informationfusion_pb_k_kernel(
         nc.vector.quantize_mx(
             out=attn_codes[:].bitcast(FP8X4), scales=attn_scales[:], in_=attn_grouped[:]
         )
+        for n in range(1, TARGET_STEP):
+            step(n)
 
         tg_words = tg[:].bitcast(F32)
-        tg_grouped = {}
+        tg_t = {}
         for b in range(B):
-            tg_t = psum_work.tile([P, TARGET_GROUPS, 2, LT], F32, tag="work")
+            tg_t[b] = psum_work.tile([P, TARGET_GROUPS, 2, LT], F32, tag="work", name="tg_t")
             for g in range(TARGET_GROUPS):
                 for u in range(2):
                     nc.tensor.transpose(
-                        tg_t[:, g, u, :],
+                        tg_t[b][:, g, u, :],
                         tg_words[:, b, g * (K_PASS // 2) + u : (g + 1) * (K_PASS // 2) : 2],
                         ident_f32[:],
                     )
-            tg_b = keep.tile(
+        step(TARGET_STEP)
+
+        tg_grouped = {}
+        for b in range(B):
+            tg_grouped[b] = keep.tile(
                 [P, TARGET_GROUPS * PACK * LT], BF16, name="tg_grouped_%d" % b, align_bytes=64
             )
             nc.scalar.copy(
-                out=tg_b[:].bitcast(F32).rearrange("p (g l u) -> p g l u", g=TARGET_GROUPS, u=2),
-                in_=tg_t[:].rearrange("p g u l -> p g l u"),
+                out=tg_grouped[b][:]
+                .bitcast(F32)
+                .rearrange("p (g l u) -> p g l u", g=TARGET_GROUPS, u=2),
+                in_=tg_t[b][:].rearrange("p g u l -> p g l u"),
             )
-            tg_grouped[b] = tg_b
-
-        bias = keep.tile([P, HALVES, PACK, P], F32)
+        bias_ps = {}
         for h in range(HALVES):
-            bias_ps = psum_work.tile([P, N_HALF], F32, tag="work")
+            bias_ps[h] = psum_work.tile([P, N_HALF], F32, tag="work", name="bias_ps")
             nc.tensor.matmul(
-                out=bias_ps[:],
+                out=bias_ps[h][:],
                 lhsT=ones[:],
                 rhs=bias_row[:, h * N_HALF : (h + 1) * N_HALF],
                 start=True,
                 stop=True,
             )
-            nc.vector.tensor_copy(
-                out=bias[:, h, :, :], in_=bias_ps[:].rearrange("l (n c) -> l c n", c=PACK)
-            )
+        step(TARGET_STEP + 1)
+
         for b in range(B):
             codes = keep.tile([P, TARGET_GROUPS * LT], U32, name="tg_codes_%d" % b, align_bytes=64)
             scales = keep.tile([P, TARGET_GROUPS * LT], U8, name="tg_scales_%d" % b, align_bytes=64)
@@ -284,24 +311,14 @@ def tile_informationfusion_pb_k_kernel(
             for g in range(TARGET_GROUPS):
                 x_codes[(g, b)] = codes[:, g * LT : (g + 1) * LT]
                 x_scales[(g, b)] = scales[:, g * LT : (g + 1) * LT]
+        bias = keep.tile([P, HALVES, PACK, P], F32)
+        for h in range(HALVES):
+            nc.scalar.copy(
+                out=bias[:, h, :, :], in_=bias_ps[h][:].rearrange("l (n c) -> l c n", c=PACK)
+            )
 
-        steady_from = first_unit[WF_FIRST_LOAD]
-        trailing_from = first_unit[last_load] - 1
-        units_per_group = LOAD_GROUPS // WF_PER_LOAD
-        for n in range(trailing_from + GROUPS - trailing_group):
-            if n + 1 < len(units):
-                regroup(n + 1)
-            if n < len(units):
-                quantise_aux(n)
-                first_product(n)
-            if 0 <= n - 1 < len(units):
-                round_x(n - 1)
-            if 0 <= n - 2 < len(units):
-                quantise_x(n - 2)
-            if n >= trailing_from:
-                second_product(trailing_group + n - trailing_from)
-            elif n >= steady_from and (n - steady_from) % units_per_group == 0:
-                second_product((n - steady_from) // units_per_group)
+        for n in range(TARGET_STEP + 2, len(units) + 3):
+            step(n)
 
         for b in range(B):
             for h in range(HALVES):

@@ -28,7 +28,7 @@ RAW_BUFS = 4
 SP_FIRST = 14
 TARGET_STEP = 4
 
-VEC_M = 76
+VEC_M = 80
 
 FLOPS = 2 * B * LT * LA * DA + 2 * B * LT * F * DT
 
@@ -54,7 +54,7 @@ def tile_informationfusion_pb_k_kernel(
         keep = ctx.enter_context(tc.tile_pool(name="keep", bufs=1))
         raw_pool = ctx.enter_context(tc.tile_pool(name="raw", bufs=RAW_BUFS))
         stage = ctx.enter_context(tc.tile_pool(name="stage", bufs=3))
-        tail = ctx.enter_context(tc.tile_pool(name="tail", bufs=2))
+        tail = ctx.enter_context(tc.tile_pool(name="tail", bufs=B * HALVES))
         psum_y = ctx.enter_context(tc.psum_pool(name="psum_y", bufs=1))
         psum_work = ctx.enter_context(tc.psum_pool(name="psum_work", bufs=4))
 

@@ -21,11 +21,12 @@ GROUPS = F // K_PASS
 TARGET_GROUPS = DT // K_PASS
 AUX_GROUPS = DA // K_PASS
 N_HALF = 512
-HALVES = DT // N_HALF
+COL_TILES = (DT - N_HALF) // P
 
 LOAD_GROUPS = 4
 RAW_BUFS = 4
-SP_FIRST = 14
+SP_FIRST = 16
+SPLIT_GROUPS = 4
 TARGET_STEP = 4
 
 VEC_M = 80
@@ -54,15 +55,15 @@ def tile_informationfusion_pb_k_kernel(
         keep = ctx.enter_context(tc.tile_pool(name="keep", bufs=1))
         raw_pool = ctx.enter_context(tc.tile_pool(name="raw", bufs=RAW_BUFS))
         stage = ctx.enter_context(tc.tile_pool(name="stage", bufs=3))
-        tail = ctx.enter_context(tc.tile_pool(name="tail", bufs=B * HALVES))
+        tail = ctx.enter_context(tc.tile_pool(name="tail", bufs=1))
         psum_y = ctx.enter_context(tc.psum_pool(name="psum_y", bufs=1))
-        psum_work = ctx.enter_context(tc.psum_pool(name="psum_work", bufs=4))
+        psum_work = ctx.enter_context(tc.psum_pool(name="psum_work", bufs=2))
 
         wf_planes = keep.tile([P, (GROUPS // 4) * DT], U8, align_bytes=64)
         nc.vector.memset(wf_planes[:].bitcast(I32), 0)
         bias_row = keep.tile([P, DT], BF16)
         nc.vector.memset(bias_row[:], 0.0)
-        ones = keep.tile([P, P], BF16)
+        ones = keep.tile([P, 1], BF16)
         nc.vector.memset(ones[:], 1.0)
         warm = keep.tile([P, 1], F32)
         nc.vector.memset(warm[:], 0.0)
@@ -80,12 +81,15 @@ def tile_informationfusion_pb_k_kernel(
         wf_queued = set()
         raw = {}
 
+        def load_wf_cols(g, first, end):
+            nc.sync.dma_start(
+                out=wf[g][:, first:end].bitcast(I32),
+                in_=Wf_words[g, :, first:end, :].rearrange("p n t -> p (n t)").bitcast(I32),
+            )
+
         def load_wf(g):
             wf_queued.add(g)
-            nc.sync.dma_start(
-                out=wf[g][:].bitcast(I32),
-                in_=Wf_words[g].rearrange("p n t -> p (n t)").bitcast(I32),
-            )
+            load_wf_cols(g, 0, DT)
 
         def load_wf_scales(block, quad):
             nc.sync.dma_start(
@@ -113,9 +117,12 @@ def tile_informationfusion_pb_k_kernel(
                 nc.sync.dma_start(out=tg[:], in_=target.rearrange("b l d -> l b d"))
                 nc.sync.dma_start(out=bias_row[0:1, :], in_=b_f.rearrange("(o n) -> o n", o=1))
             if k == last_load:
-                for g in range(GROUPS):
+                for g in range(GROUPS - SPLIT_GROUPS):
                     if g not in wf_queued:
                         load_wf(g)
+                for first in (0, N_HALF):
+                    for g in range(GROUPS - SPLIT_GROUPS, GROUPS):
+                        load_wf_cols(g, first, first + N_HALF)
 
         for k in range(RAW_BUFS):
             load_aux(k)
@@ -125,8 +132,12 @@ def tile_informationfusion_pb_k_kernel(
         aux_scales = {}
         banks = {}
         x_grouped = {}
-        x_codes = {}
-        x_scales = {}
+        x_codes = [
+            keep.tile([P, B * LT], U32, name="x_codes_%d" % g, align_bytes=64) for g in range(GROUPS)
+        ]
+        x_scales = [
+            keep.tile([P, B * LT], U8, name="x_scales_%d" % g, align_bytes=64) for g in range(GROUPS)
+        ]
 
         def regroup(u):
             k, place, b, g = units[u]
@@ -174,29 +185,37 @@ def tile_informationfusion_pb_k_kernel(
 
         def quantise_x(u):
             k, place, b, g = units[u]
-            codes = keep.tile([P, LT], U32, name="x_codes_%d_%d" % (g, b), align_bytes=64)
-            scales = keep.tile([P, LT], U8, name="x_scales_%d_%d" % (g, b), align_bytes=64)
             nc.vector.quantize_mx(
-                out=codes[:].bitcast(FP8X4), scales=scales[:], in_=x_grouped[u][:]
+                out=x_codes[g][:, b * LT : (b + 1) * LT].bitcast(FP8X4),
+                scales=x_scales[g][:, b * LT : (b + 1) * LT],
+                in_=x_grouped[u][:],
             )
-            x_codes[(g, b)] = codes[:]
-            x_scales[(g, b)] = scales[:]
 
-        y = {}
-        for b in range(B):
-            for h in range(HALVES):
-                y[(b, h)] = psum_y.tile([P, N_HALF], F32, name="y_%d_%d" % (b, h))
+        y_rows = {}
+        y_cols = {}
 
-        def second_product(g, b):
-            first_row = 4 * (g % 4)
-            for h in range(HALVES):
-                plane_col = (g // 4) * DT + h * N_HALF
+        def second_rows(g, b):
+            plane_col = (g // 4) * DT
+            nc.tensor.matmul_mx(
+                out=y_rows[b][:],
+                lhsT=x_codes[g][:, b * LT : (b + 1) * LT].bitcast(FP8X4),
+                lhsT_scale=x_scales[g][:, b * LT : (b + 1) * LT],
+                rhs=wf[g][:, 0:N_HALF].bitcast(FP8X4),
+                rhs_scale=wf_planes[4 * (g % 4) : P, plane_col : plane_col + N_HALF],
+                start=(g == 0),
+                stop=(g == GROUPS - 1),
+            )
+
+        def second_cols(g):
+            for i in range(COL_TILES):
+                first = N_HALF + i * P
+                plane_col = (g // 4) * DT + first
                 nc.tensor.matmul_mx(
-                    out=y[(b, h)][:],
-                    lhsT=x_codes[(g, b)].bitcast(FP8X4),
-                    lhsT_scale=x_scales[(g, b)],
-                    rhs=wf[g][:, h * N_HALF : (h + 1) * N_HALF].bitcast(FP8X4),
-                    rhs_scale=wf_planes[first_row:P, plane_col : plane_col + N_HALF],
+                    out=y_cols[i][:],
+                    lhsT=wf[g][:, first : first + P].bitcast(FP8X4),
+                    lhsT_scale=wf_planes[4 * (g % 4) : P, plane_col : plane_col + P],
+                    rhs=x_codes[g][:].bitcast(FP8X4),
+                    rhs_scale=x_scales[g][:],
                     start=(g == 0),
                     stop=(g == GROUPS - 1),
                 )
@@ -219,7 +238,10 @@ def tile_informationfusion_pb_k_kernel(
             for g in range(GROUPS):
                 for b in range(B):
                     if max(SP_FIRST + g, x_step.get((g, b), 0)) == n:
-                        second_product(g, b)
+                        second_rows(g, b)
+                if g < GROUPS - SPLIT_GROUPS:
+                    if max([SP_FIRST + g] + [x_step.get((g, b), 0) for b in range(B)]) == n:
+                        second_cols(g)
 
         row_max = keep.tile([P, B], F32)
         nc.vector.reduce_max(out=row_max[:], in_=sc[:], axis=mybir.AxisListType.X)
@@ -269,7 +291,9 @@ def tile_informationfusion_pb_k_kernel(
         tg_words = tg[:].bitcast(F32)
         tg_t = {}
         for b in range(B):
-            tg_t[b] = psum_work.tile([P, TARGET_GROUPS, 2, LT], F32, tag="work", name="tg_t")
+            tg_t[b] = psum_y.tile(
+                [P, TARGET_GROUPS, 2, LT], F32, tag="y_cols_%d" % b, name="tg_t_%d" % b
+            )
             for g in range(TARGET_GROUPS):
                 for u in range(2):
                     nc.tensor.transpose(
@@ -277,66 +301,85 @@ def tile_informationfusion_pb_k_kernel(
                         tg_words[:, b, g * (K_PASS // 2) + u : (g + 1) * (K_PASS // 2) : 2],
                         ident_f32[:],
                     )
-        step(TARGET_STEP)
-
-        tg_grouped = {}
-        for b in range(B):
-            tg_grouped[b] = keep.tile(
-                [P, TARGET_GROUPS * PACK * LT], BF16, name="tg_grouped_%d" % b, align_bytes=64
-            )
-            nc.scalar.copy(
-                out=tg_grouped[b][:]
-                .bitcast(F32)
-                .rearrange("p (g l u) -> p g l u", g=TARGET_GROUPS, u=2),
-                in_=tg_t[b][:].rearrange("p g u l -> p g l u"),
-            )
-        bias_ps = {}
-        for h in range(HALVES):
-            bias_ps[h] = psum_work.tile([P, N_HALF], F32, tag="work", name="bias_ps")
+        bias_ps = psum_y.tile([P, PACK + COL_TILES], F32, tag="y_cols_2", name="bias_ps")
+        for c in range(PACK):
             nc.tensor.matmul(
-                out=bias_ps[h][:],
-                lhsT=ones[:],
-                rhs=bias_row[:, h * N_HALF : (h + 1) * N_HALF],
+                out=bias_ps[:, c : c + 1],
+                lhsT=bias_row[:, c:N_HALF:PACK],
+                rhs=ones[:],
                 start=True,
                 stop=True,
             )
+        for i in range(COL_TILES):
+            nc.tensor.matmul(
+                out=bias_ps[:, PACK + i : PACK + i + 1],
+                lhsT=bias_row[:, N_HALF + i * P : N_HALF + (i + 1) * P],
+                rhs=ones[:],
+                start=True,
+                stop=True,
+            )
+        step(TARGET_STEP)
+
+        tg_grouped = keep.tile([P, TARGET_GROUPS, B, LT * PACK], BF16, align_bytes=64)
+        for b in range(B):
+            nc.scalar.copy(
+                out=tg_grouped[:, :, b, :].bitcast(F32).rearrange("p g (l u) -> p g l u", u=2),
+                in_=tg_t[b][:].rearrange("p g u l -> p g l u"),
+            )
+        bias_col = keep.tile([P, PACK + COL_TILES], F32)
+        nc.scalar.copy(out=bias_col[:], in_=bias_ps[:])
         step(TARGET_STEP + 1)
 
-        for b in range(B):
-            codes = keep.tile([P, TARGET_GROUPS * LT], U32, name="tg_codes_%d" % b, align_bytes=64)
-            scales = keep.tile([P, TARGET_GROUPS * LT], U8, name="tg_scales_%d" % b, align_bytes=64)
+        for g in range(TARGET_GROUPS):
             nc.vector.quantize_mx(
-                out=codes[:].bitcast(FP8X4), scales=scales[:], in_=tg_grouped[b][:]
+                out=x_codes[g][:].bitcast(FP8X4),
+                scales=x_scales[g][:],
+                in_=tg_grouped[:, g, :, :].rearrange("p b w -> p (b w)"),
             )
-            for g in range(TARGET_GROUPS):
-                x_codes[(g, b)] = codes[:, g * LT : (g + 1) * LT]
-                x_scales[(g, b)] = scales[:, g * LT : (g + 1) * LT]
-        bias = keep.tile([P, HALVES, PACK, P], F32)
-        for h in range(HALVES):
-            nc.scalar.copy(
-                out=bias[:, h, :, :], in_=bias_ps[h][:].rearrange("l (n c) -> l c n", c=PACK)
-            )
+        for b in range(B):
+            y_rows[b] = psum_y.tile([P, N_HALF], F32, name="y_rows_%d" % b)
+        for i in range(COL_TILES):
+            y_cols[i] = psum_y.tile([P, B * LT], F32, name="y_cols_%d" % i, tag="y_cols_%d" % i)
 
-        for n in range(TARGET_STEP + 2, len(units) + 3):
+        for n in range(TARGET_STEP + 2, max(len(units) + 3, SP_FIRST + GROUPS)):
             step(n)
 
+        def copy_rows(b):
+            y_sb = tail.tile([P, PACK, P], F32, name="y_sb_%d" % b)
+            nc.vector.tensor_copy(out=y_sb[:], in_=y_rows[b][:].rearrange("l (n c) -> l c n", c=PACK))
+            return y_sb
+
+        def finish_rows(b, y_sb):
+            y_t = psum_work.tile([P, PACK, LT], F32, tag="work")
+            for c in range(PACK):
+                nc.tensor.transpose(y_t[:, c, :], y_sb[:, c, :], ident_f32[:])
+            o_sb = tail.tile([P, PACK, LT], F32, name="o_rows_%d" % b)
+            for c in range(PACK):
+                nc.scalar.activation(
+                    out=o_sb[:, c, :], in_=y_t[:, c, :], func=ACT.Tanh, bias=bias_col[:, c : c + 1], scale=1.0
+                )
+            nc.sync.dma_start(
+                out=out[b, 0:N_HALF, :].rearrange("(n c) l -> n (c l)", c=PACK),
+                in_=o_sb[:].rearrange("n c l -> n (c l)"),
+            )
+
+        y_sb = [copy_rows(b) for b in range(B)]
+        split = range(GROUPS - SPLIT_GROUPS, GROUPS)
+        second_cols(split[0])
         for b in range(B):
-            for h in range(HALVES):
-                y_sb = tail.tile([P, PACK, P], F32, tag="y_sb")
-                nc.vector.tensor_tensor(
-                    out=y_sb[:],
-                    in0=y[(b, h)][:].rearrange("l (n c) -> l c n", c=PACK),
-                    in1=bias[:, h, :, :],
-                    op=mybir.AluOpType.add,
-                )
-                y_t = psum_work.tile([P, PACK, LT], F32, tag="work")
-                for c in range(PACK):
-                    nc.tensor.transpose(y_t[:, c, :], y_sb[:, c, :], ident_f32[:])
-                o_sb = tail.tile([P, PACK, LT], F32, tag="o_sb")
-                nc.scalar.activation(out=o_sb[:], in_=y_t[:], func=ACT.Tanh)
-                nc.sync.dma_start(
-                    out=out[b, h * N_HALF : (h + 1) * N_HALF, :].rearrange(
-                        "(n c) l -> n (c l)", c=PACK
-                    ),
-                    in_=o_sb[:].rearrange("n c l -> n (c l)"),
-                )
+            finish_rows(b, y_sb[b])
+        for g in split[1:]:
+            second_cols(g)
+        for i in range(COL_TILES):
+            o_sb = tail.tile([P, B, LT], F32, name="o_cols_%d" % i)
+            nc.scalar.activation(
+                out=o_sb[:],
+                in_=y_cols[i][:].rearrange("p (b l) -> p b l", b=B),
+                func=ACT.Tanh,
+                bias=bias_col[:, PACK + i : PACK + i + 1],
+                scale=1.0,
+            )
+            first = N_HALF + i * P
+            nc.sync.dma_start(
+                out=out[:, first : first + P, :].rearrange("b n l -> n b l"), in_=o_sb[:]
+            )

@@ -27,7 +27,7 @@ LOAD_GROUPS = 4
 RAW_BUFS = 4
 SP_FIRST = 16
 SPLIT_GROUPS = 4
-TARGET_STEP = 4
+TARGET_STEP = 6
 
 VEC_M = 80
 
@@ -74,7 +74,8 @@ def tile_informationfusion_pb_k_kernel(
         make_identity(nc, ident_f32[:])
 
         sc = keep.tile([P, B, LA], BF16)
-        nc.sync.dma_start(out=sc[:], in_=scores.rearrange("b l a -> l b a"))
+        for b in range(B):
+            nc.sync.dma_start(out=sc[:, b, :], in_=scores[b])
         tg = keep.tile([P, B, DT], BF16)
 
         wf = [keep.tile([P, DT], U32, name="wf%d" % g, align_bytes=64) for g in range(GROUPS)]
@@ -87,9 +88,6 @@ def tile_informationfusion_pb_k_kernel(
                 in_=Wf_words[g, :, first:end, :].rearrange("p n t -> p (n t)").bitcast(I32),
             )
 
-        def load_wf(g):
-            wf_queued.add(g)
-            load_wf_cols(g, 0, DT)
 
         def load_wf_scales(block, quad):
             nc.sync.dma_start(
@@ -97,10 +95,17 @@ def tile_informationfusion_pb_k_kernel(
                 in_=Wf_scales[4 * block : 4 * block + 4, 4 * quad : 4 * quad + 4, :].bitcast(I32),
             )
 
+        def load_wf(g, first, end):
+            if g % 4 == 0 and g not in wf_queued:
+                for quad in range(4):
+                    load_wf_scales(g // 4, quad)
+            wf_queued.add(g)
+            load_wf_cols(g, first, end)
+
         def load_aux(k):
             for g in range(GROUPS):
                 if g not in wf_queued and SP_FIRST + g < first_unit[k] - 2:
-                    load_wf(g)
+                    load_wf(g, 0, DT)
             start, end, b = loads[k]
             raw_k = raw_pool.tile([P, PACK, (end - start) * K_PASS], BF16, tag="raw")
             nc.sync.dma_start(
@@ -110,19 +115,16 @@ def tile_informationfusion_pb_k_kernel(
                 ),
             )
             raw[k] = raw_k
-            if k < GROUPS // 4:
-                for quad in range(4):
-                    load_wf_scales(k, quad)
-            if k == B - 1:
+            if k == B:
                 nc.sync.dma_start(out=tg[:], in_=target.rearrange("b l d -> l b d"))
                 nc.sync.dma_start(out=bias_row[0:1, :], in_=b_f.rearrange("(o n) -> o n", o=1))
             if k == last_load:
                 for g in range(GROUPS - SPLIT_GROUPS):
                     if g not in wf_queued:
-                        load_wf(g)
+                        load_wf(g, 0, DT)
                 for first in (0, N_HALF):
                     for g in range(GROUPS - SPLIT_GROUPS, GROUPS):
-                        load_wf_cols(g, first, first + N_HALF)
+                        load_wf(g, first, first + N_HALF)
 
         for k in range(RAW_BUFS):
             load_aux(k)
@@ -244,12 +246,18 @@ def tile_informationfusion_pb_k_kernel(
                         second_cols(g)
 
         row_max = keep.tile([P, B], F32)
-        nc.vector.reduce_max(out=row_max[:], in_=sc[:], axis=mybir.AxisListType.X)
         neg_max = keep.tile([P, B], F32)
-        nc.vector.tensor_scalar_mul(out=neg_max[:], in0=row_max[:], scalar1=-1.0)
         expo = keep.tile([P, B, LA], F32)
         row_sum = keep.tile([P, B], F32)
+        inv_sum = keep.tile([P, B], F32)
+        attn = keep.tile([P, B, PACK, P], BF16)
         for b in range(B):
+            nc.vector.reduce_max(
+                out=row_max[:, b : b + 1], in_=sc[:, b, :], axis=mybir.AxisListType.X
+            )
+            nc.vector.tensor_scalar_mul(
+                out=neg_max[:, b : b + 1], in0=row_max[:, b : b + 1], scalar1=-1.0
+            )
             nc.scalar.activation(
                 out=expo[:, b, :],
                 in_=sc[:, b, :],
@@ -258,16 +266,14 @@ def tile_informationfusion_pb_k_kernel(
                 scale=1.0,
                 accum_out=row_sum[:, b : b + 1],
             )
-        regroup(0)
-        inv_sum = keep.tile([P, B], F32)
-        nc.vector.reciprocal(out=inv_sum[:], in_=row_sum[:])
-        attn = keep.tile([P, B, PACK, P], BF16)
         for b in range(B):
+            nc.vector.reciprocal(out=inv_sum[:, b : b + 1], in_=row_sum[:, b : b + 1])
             nc.vector.tensor_scalar_mul(
                 out=attn[:, b, :, :],
                 in0=expo[:, b, :].rearrange("l (p j) -> l j p", j=PACK),
                 scalar1=inv_sum[:, b : b + 1],
             )
+        regroup(0)
         step(0)
         attn_grouped = keep.tile([P, B * PACK * LT], BF16, align_bytes=64)
         for b in range(B):

@@ -23,11 +23,12 @@ AUX_GROUPS = DA // K_PASS
 N_HALF = 512
 COL_TILES = (DT - N_HALF) // P
 
-LOAD_GROUPS = 4
-RAW_BUFS = 4
+SHORT_LOADS = ((0, 3), (1, 4))
+LONG_LOADS = ((0, 5), (1, 5), (0, 6), (1, 5))
+LONG_BUFS = 3
 SP_FIRST = 16
 SPLIT_GROUPS = 4
-TARGET_STEP = 6
+TARGET_STEP = 8
 
 VEC_M = 80
 
@@ -39,9 +40,12 @@ def tile_informationfusion_pb_k_kernel(
 ):
     nc = tc.nc
 
-    starts = [0] + list(range(AUX_GROUPS % LOAD_GROUPS, AUX_GROUPS, LOAD_GROUPS))
-    ends = starts[1:] + [AUX_GROUPS]
-    loads = [(start, end, b) for start, end in zip(starts, ends) for b in range(B)]
+    loads = []
+    groups_queued = [0] * B
+    for b, count in SHORT_LOADS + LONG_LOADS:
+        loads.append((groups_queued[b], groups_queued[b] + count, b))
+        groups_queued[b] += count
+    assert groups_queued == [AUX_GROUPS] * B
     units = []
     first_unit = {}
     for k, (start, end, b) in enumerate(loads):
@@ -53,9 +57,9 @@ def tile_informationfusion_pb_k_kernel(
     with ExitStack() as ctx:
         ctx.enter_context(tc.manual_schedule())
         keep = ctx.enter_context(tc.tile_pool(name="keep", bufs=1))
-        raw_pool = ctx.enter_context(tc.tile_pool(name="raw", bufs=RAW_BUFS))
+        short_pool = ctx.enter_context(tc.tile_pool(name="short", bufs=len(SHORT_LOADS)))
+        long_pool = ctx.enter_context(tc.tile_pool(name="long", bufs=LONG_BUFS))
         stage = ctx.enter_context(tc.tile_pool(name="stage", bufs=3))
-        tail = ctx.enter_context(tc.tile_pool(name="tail", bufs=1))
         psum_y = ctx.enter_context(tc.psum_pool(name="psum_y", bufs=1))
         psum_work = ctx.enter_context(tc.psum_pool(name="psum_work", bufs=2))
 
@@ -107,7 +111,8 @@ def tile_informationfusion_pb_k_kernel(
                 if g not in wf_queued and SP_FIRST + g < first_unit[k] - 2:
                     load_wf(g, 0, DT)
             start, end, b = loads[k]
-            raw_k = raw_pool.tile([P, PACK, (end - start) * K_PASS], BF16, tag="raw")
+            pool = short_pool if k < len(SHORT_LOADS) else long_pool
+            raw_k = pool.tile([P, PACK, (end - start) * K_PASS], BF16, tag="raw")
             nc.sync.dma_start(
                 out=raw_k[:],
                 in_=auxiliary[b, :, start * K_PASS : end * K_PASS].rearrange(
@@ -115,7 +120,7 @@ def tile_informationfusion_pb_k_kernel(
                 ),
             )
             raw[k] = raw_k
-            if k == B:
+            if k == 2:
                 nc.sync.dma_start(out=tg[:], in_=target.rearrange("b l d -> l b d"))
                 nc.sync.dma_start(out=bias_row[0:1, :], in_=b_f.rearrange("(o n) -> o n", o=1))
             if k == last_load:
@@ -126,7 +131,7 @@ def tile_informationfusion_pb_k_kernel(
                     for g in range(GROUPS - SPLIT_GROUPS, GROUPS):
                         load_wf(g, first, first + N_HALF)
 
-        for k in range(RAW_BUFS):
+        for k in range(len(SHORT_LOADS) + LONG_BUFS):
             load_aux(k)
 
         grouped = {}
@@ -152,8 +157,8 @@ def tile_informationfusion_pb_k_kernel(
             nc.scalar.copy(out=dst[:, VEC_M:P, :, :], in_=src[:, VEC_M:P, :, :])
             grouped[u] = grouped_u
             if u + 1 == len(units) or units[u + 1][0] != k:
-                if k + RAW_BUFS <= last_load:
-                    load_aux(k + RAW_BUFS)
+                if k >= len(SHORT_LOADS) and k + LONG_BUFS <= last_load:
+                    load_aux(k + LONG_BUFS)
 
         def quantise_aux(u):
             codes = stage.tile([P, K_PASS], U32, tag="aux_codes", align_bytes=64)
@@ -208,19 +213,18 @@ def tile_informationfusion_pb_k_kernel(
                 stop=(g == GROUPS - 1),
             )
 
-        def second_cols(g):
-            for i in range(COL_TILES):
-                first = N_HALF + i * P
-                plane_col = (g // 4) * DT + first
-                nc.tensor.matmul_mx(
-                    out=y_cols[i][:],
-                    lhsT=wf[g][:, first : first + P].bitcast(FP8X4),
-                    lhsT_scale=wf_planes[4 * (g % 4) : P, plane_col : plane_col + P],
-                    rhs=x_codes[g][:].bitcast(FP8X4),
-                    rhs_scale=x_scales[g][:],
-                    start=(g == 0),
-                    stop=(g == GROUPS - 1),
-                )
+        def second_cols(g, i):
+            first = N_HALF + i * P
+            plane_col = (g // 4) * DT + first
+            nc.tensor.matmul_mx(
+                out=y_cols[i][:],
+                lhsT=wf[g][:, first : first + P].bitcast(FP8X4),
+                lhsT_scale=wf_planes[4 * (g % 4) : P, plane_col : plane_col + P],
+                rhs=x_codes[g][:].bitcast(FP8X4),
+                rhs_scale=x_scales[g][:],
+                start=(g == 0),
+                stop=(g == GROUPS - 1),
+            )
 
         x_step = {}
         for u, (k, place, b, g) in enumerate(units):
@@ -237,17 +241,17 @@ def tile_informationfusion_pb_k_kernel(
                 round_x(n - 2)
             if 0 <= n - 3 < len(units):
                 quantise_x(n - 3)
-            for g in range(GROUPS):
+            for g in range(GROUPS - SPLIT_GROUPS):
                 for b in range(B):
                     if max(SP_FIRST + g, x_step.get((g, b), 0)) == n:
                         second_rows(g, b)
-                if g < GROUPS - SPLIT_GROUPS:
-                    if max([SP_FIRST + g] + [x_step.get((g, b), 0) for b in range(B)]) == n:
-                        second_cols(g)
+                if max([SP_FIRST + g] + [x_step.get((g, b), 0) for b in range(B)]) == n:
+                    for i in range(COL_TILES):
+                        second_cols(g, i)
 
         row_max = keep.tile([P, B], F32)
         neg_max = keep.tile([P, B], F32)
-        expo = keep.tile([P, B, LA], F32)
+        expo = keep.tile([P, B, LA], F32, tag="wide", name="expo", align_bytes=64)
         row_sum = keep.tile([P, B], F32)
         inv_sum = keep.tile([P, B], F32)
         attn = keep.tile([P, B, PACK, P], BF16)
@@ -326,7 +330,9 @@ def tile_informationfusion_pb_k_kernel(
             )
         step(TARGET_STEP)
 
-        tg_grouped = keep.tile([P, TARGET_GROUPS, B, LT * PACK], BF16, align_bytes=64)
+        tg_grouped = keep.tile(
+            [P, TARGET_GROUPS, B, LT * PACK], BF16, tag="wide", name="tg_grouped", align_bytes=64
+        )
         for b in range(B):
             nc.scalar.copy(
                 out=tg_grouped[:, :, b, :].bitcast(F32).rearrange("p g (l u) -> p g l u", u=2),
@@ -347,39 +353,47 @@ def tile_informationfusion_pb_k_kernel(
         for i in range(COL_TILES):
             y_cols[i] = psum_y.tile([P, B * LT], F32, name="y_cols_%d" % i, tag="y_cols_%d" % i)
 
-        for n in range(TARGET_STEP + 2, max(len(units) + 3, SP_FIRST + GROUPS)):
+        for n in range(TARGET_STEP + 2, max(len(units) + 3, SP_FIRST + GROUPS - SPLIT_GROUPS)):
             step(n)
 
+        rows_sb = short_pool.tile([P, B, 2, PACK, LT], F32, tag="raw", name="rows_sb")
+        cols_sb = short_pool.tile([P, COL_TILES, B, LT], F32, tag="raw", name="cols_sb")
+
         def copy_rows(b):
-            y_sb = tail.tile([P, PACK, P], F32, name="y_sb_%d" % b)
-            nc.vector.tensor_copy(out=y_sb[:], in_=y_rows[b][:].rearrange("l (n c) -> l c n", c=PACK))
+            y_sb = rows_sb[:, b, 0, :, :]
+            nc.vector.tensor_copy(out=y_sb, in_=y_rows[b][:].rearrange("l (n c) -> l c n", c=PACK))
             return y_sb
 
         def finish_rows(b, y_sb):
             y_t = psum_work.tile([P, PACK, LT], F32, tag="work")
             for c in range(PACK):
                 nc.tensor.transpose(y_t[:, c, :], y_sb[:, c, :], ident_f32[:])
-            o_sb = tail.tile([P, PACK, LT], F32, name="o_rows_%d" % b)
+            o_sb = rows_sb[:, b, 1, :, :]
             for c in range(PACK):
                 nc.scalar.activation(
                     out=o_sb[:, c, :], in_=y_t[:, c, :], func=ACT.Tanh, bias=bias_col[:, c : c + 1], scale=1.0
                 )
             nc.sync.dma_start(
                 out=out[b, 0:N_HALF, :].rearrange("(n c) l -> n (c l)", c=PACK),
-                in_=o_sb[:].rearrange("n c l -> n (c l)"),
+                in_=o_sb.rearrange("n c l -> n (c l)"),
             )
 
-        y_sb = [copy_rows(b) for b in range(B)]
         split = range(GROUPS - SPLIT_GROUPS, GROUPS)
-        second_cols(split[0])
+        y_sb = {}
+        for b in range(B):
+            for g in split:
+                second_rows(g, b)
+            y_sb[b] = copy_rows(b)
+        for i in range(COL_TILES):
+            second_cols(split[0], i)
         for b in range(B):
             finish_rows(b, y_sb[b])
-        for g in split[1:]:
-            second_cols(g)
         for i in range(COL_TILES):
-            o_sb = tail.tile([P, B, LT], F32, name="o_cols_%d" % i)
+            for g in split[1:]:
+                second_cols(g, i)
+            o_sb = cols_sb[:, i, :, :]
             nc.scalar.activation(
-                out=o_sb[:],
+                out=o_sb,
                 in_=y_cols[i][:].rearrange("p (b l) -> p b l", b=B),
                 func=ACT.Tanh,
                 bias=bias_col[:, PACK + i : PACK + i + 1],
@@ -387,5 +401,5 @@ def tile_informationfusion_pb_k_kernel(
             )
             first = N_HALF + i * P
             nc.sync.dma_start(
-                out=out[:, first : first + P, :].rearrange("b n l -> n b l"), in_=o_sb[:]
+                out=out[:, first : first + P, :].rearrange("b n l -> n b l"), in_=o_sb
             )

@@ -24,13 +24,13 @@ N_HALF = 512
 COL_TILES = (DT - N_HALF) // P
 
 SHORT_LOADS = ((0, 3), (1, 4))
-LONG_LOADS = ((0, 5), (1, 5), (0, 6), (1, 5))
+LONG_LOADS = ((0, 5), (1, 6), (0, 6), (1, 4))
 LONG_BUFS = 3
 SP_FIRST = 16
 SPLIT_GROUPS = 4
 TARGET_STEP = 8
 
-VEC_M = 80
+VEC_M = 76
 
 FLOPS = 2 * B * LT * LA * DA + 2 * B * LT * F * DT
 
@@ -108,7 +108,7 @@ def tile_informationfusion_pb_k_kernel(
 
         def load_aux(k):
             for g in range(GROUPS):
-                if g not in wf_queued and SP_FIRST + g < first_unit[k] - 2:
+                if g not in wf_queued and SP_FIRST + g < first_unit[k] - 1:
                     load_wf(g, 0, DT)
             start, end, b = loads[k]
             pool = short_pool if k < len(SHORT_LOADS) else long_pool
@@ -379,15 +379,16 @@ def tile_informationfusion_pb_k_kernel(
             )
 
         split = range(GROUPS - SPLIT_GROUPS, GROUPS)
-        y_sb = {}
-        for b in range(B):
-            for g in split:
+        for g in split:
+            for b in range(B):
                 second_rows(g, b)
-            y_sb[b] = copy_rows(b)
-        for i in range(COL_TILES):
+        y_sb = [copy_rows(b) for b in range(B)]
+        for i in range(0, COL_TILES // 2):
             second_cols(split[0], i)
         for b in range(B):
             finish_rows(b, y_sb[b])
+        for i in range(COL_TILES // 2, COL_TILES):
+            second_cols(split[0], i)
         for i in range(COL_TILES):
             for g in split[1:]:
                 second_cols(g, i)

@@ -28,6 +28,7 @@ LONG_LOADS = ((0, 5), (1, 6), (0, 6), (1, 4))
 LONG_BUFS = 3
 SP_FIRST = 16
 SPLIT_GROUPS = 4
+TAIL_GROUPS = 5
 TARGET_STEP = 8
 
 VEC_M = 76
@@ -241,7 +242,7 @@ def tile_informationfusion_pb_k_kernel(
                 round_x(n - 2)
             if 0 <= n - 3 < len(units):
                 quantise_x(n - 3)
-            for g in range(GROUPS - SPLIT_GROUPS):
+            for g in range(GROUPS - TAIL_GROUPS):
                 for b in range(B):
                     if max(SP_FIRST + g, x_step.get((g, b), 0)) == n:
                         second_rows(g, b)
@@ -353,7 +354,7 @@ def tile_informationfusion_pb_k_kernel(
         for i in range(COL_TILES):
             y_cols[i] = psum_y.tile([P, B * LT], F32, name="y_cols_%d" % i, tag="y_cols_%d" % i)
 
-        for n in range(TARGET_STEP + 2, max(len(units) + 3, SP_FIRST + GROUPS - SPLIT_GROUPS)):
+        for n in range(TARGET_STEP + 2, max(len(units) + 3, SP_FIRST + GROUPS - TAIL_GROUPS)):
             step(n)
 
         rows_sb = short_pool.tile([P, B, 2, PACK, LT], F32, tag="raw", name="rows_sb")
@@ -378,19 +379,17 @@ def tile_informationfusion_pb_k_kernel(
                 in_=o_sb.rearrange("n c l -> n (c l)"),
             )
 
-        split = range(GROUPS - SPLIT_GROUPS, GROUPS)
-        for g in split:
+        last_groups = range(GROUPS - TAIL_GROUPS, GROUPS)
+        for g in last_groups:
             for b in range(B):
                 second_rows(g, b)
         y_sb = [copy_rows(b) for b in range(B)]
-        for i in range(0, COL_TILES // 2):
-            second_cols(split[0], i)
+        for i in range(COL_TILES):
+            second_cols(last_groups[0], i)
         for b in range(B):
             finish_rows(b, y_sb[b])
-        for i in range(COL_TILES // 2, COL_TILES):
-            second_cols(split[0], i)
         for i in range(COL_TILES):
-            for g in split[1:]:
+            for g in last_groups[1:]:
                 second_cols(g, i)
             o_sb = cols_sb[:, i, :, :]
             nc.scalar.activation(

@@ -23,9 +23,7 @@ AUX_GROUPS = DA // K_PASS
 N_HALF = 512
 COL_TILES = (DT - N_HALF) // P
 
-SHORT_LOADS = ((0, 3), (1, 4))
-LONG_LOADS = ((0, 5), (1, 6), (0, 6), (1, 4))
-LONG_BUFS = 3
+LOADS = ((0, 3), (1, 5), (0, 7), (1, 9), (0, 4))
 SP_FIRST = 16
 SPLIT_GROUPS = 4
 TAIL_GROUPS = 5
@@ -43,7 +41,7 @@ def tile_informationfusion_pb_k_kernel(
 
     loads = []
     groups_queued = [0] * B
-    for b, count in SHORT_LOADS + LONG_LOADS:
+    for b, count in LOADS:
         loads.append((groups_queued[b], groups_queued[b] + count, b))
         groups_queued[b] += count
     assert groups_queued == [AUX_GROUPS] * B
@@ -58,9 +56,8 @@ def tile_informationfusion_pb_k_kernel(
     with ExitStack() as ctx:
         ctx.enter_context(tc.manual_schedule())
         keep = ctx.enter_context(tc.tile_pool(name="keep", bufs=1))
-        short_pool = ctx.enter_context(tc.tile_pool(name="short", bufs=len(SHORT_LOADS)))
-        long_pool = ctx.enter_context(tc.tile_pool(name="long", bufs=LONG_BUFS))
         stage = ctx.enter_context(tc.tile_pool(name="stage", bufs=3))
+        stage_x = ctx.enter_context(tc.tile_pool(name="stage_x", bufs=2))
         psum_y = ctx.enter_context(tc.psum_pool(name="psum_y", bufs=1))
         psum_work = ctx.enter_context(tc.psum_pool(name="psum_work", bufs=2))
 
@@ -78,7 +75,7 @@ def tile_informationfusion_pb_k_kernel(
         ident_f32 = keep.tile([P, P], F32)
         make_identity(nc, ident_f32[:])
 
-        sc = keep.tile([P, B, LA], BF16)
+        sc = keep.tile([P, B, LA], BF16, tag="sc_attn", align_bytes=64)
         for b in range(B):
             nc.sync.dma_start(out=sc[:, b, :], in_=scores[b])
         tg = keep.tile([P, B, DT], BF16)
@@ -112,8 +109,7 @@ def tile_informationfusion_pb_k_kernel(
                 if g not in wf_queued and SP_FIRST + g < first_unit[k] - 1:
                     load_wf(g, 0, DT)
             start, end, b = loads[k]
-            pool = short_pool if k < len(SHORT_LOADS) else long_pool
-            raw_k = pool.tile([P, PACK, (end - start) * K_PASS], BF16, tag="raw")
+            raw_k = keep.tile([P, PACK, (end - start) * K_PASS], BF16, name="raw_%d" % k, tag="raw_%d" % k)
             nc.sync.dma_start(
                 out=raw_k[:],
                 in_=auxiliary[b, :, start * K_PASS : end * K_PASS].rearrange(
@@ -132,7 +128,7 @@ def tile_informationfusion_pb_k_kernel(
                     for g in range(GROUPS - SPLIT_GROUPS, GROUPS):
                         load_wf(g, first, first + N_HALF)
 
-        for k in range(len(SHORT_LOADS) + LONG_BUFS):
+        for k in range(len(loads)):
             load_aux(k)
 
         grouped = {}
@@ -157,9 +153,6 @@ def tile_informationfusion_pb_k_kernel(
             nc.vector.tensor_copy(out=dst[:, 0:VEC_M, :, :], in_=src[:, 0:VEC_M, :, :])
             nc.scalar.copy(out=dst[:, VEC_M:P, :, :], in_=src[:, VEC_M:P, :, :])
             grouped[u] = grouped_u
-            if u + 1 == len(units) or units[u + 1][0] != k:
-                if k >= len(SHORT_LOADS) and k + LONG_BUFS <= last_load:
-                    load_aux(k + LONG_BUFS)
 
         def quantise_aux(u):
             codes = stage.tile([P, K_PASS], U32, tag="aux_codes", align_bytes=64)
@@ -184,7 +177,7 @@ def tile_informationfusion_pb_k_kernel(
             banks[u] = bank
 
         def round_x(u):
-            x_u = stage.tile([P, PACK * LT], BF16, tag="x_grouped", align_bytes=64)
+            x_u = stage_x.tile([P, PACK * LT], BF16, tag="x_grouped", align_bytes=64)
             nc.scalar.copy(
                 out=x_u[:].rearrange("p (l t) -> p l t", t=PACK),
                 in_=banks[u][:].rearrange("p t l -> p l t"),
@@ -232,7 +225,8 @@ def tile_informationfusion_pb_k_kernel(
             x_step[(g, b)] = u + 3
 
         def step(n):
-            if n + 1 < len(units):
+            new_load = n + 1 < len(units) and units[n + 1][0] != units[n][0]
+            if n + 1 < len(units) and not new_load:
                 regroup(n + 1)
             if n < len(units):
                 quantise_aux(n)
@@ -242,6 +236,8 @@ def tile_informationfusion_pb_k_kernel(
                 round_x(n - 2)
             if 0 <= n - 3 < len(units):
                 quantise_x(n - 3)
+            if new_load:
+                regroup(n + 1)
             for g in range(GROUPS - TAIL_GROUPS):
                 for b in range(B):
                     if max(SP_FIRST + g, x_step.get((g, b), 0)) == n:
@@ -280,7 +276,9 @@ def tile_informationfusion_pb_k_kernel(
             )
         regroup(0)
         step(0)
-        attn_grouped = keep.tile([P, B * PACK * LT], BF16, align_bytes=64)
+        attn_grouped = keep.tile(
+            [P, B * PACK * LT], BF16, tag="sc_attn", name="attn_grouped", align_bytes=64
+        )
         for b in range(B):
             attn_t = psum_work.tile([P, PACK, LT], BF16, tag="work")
             for j in range(PACK):
@@ -357,8 +355,8 @@ def tile_informationfusion_pb_k_kernel(
         for n in range(TARGET_STEP + 2, max(len(units) + 3, SP_FIRST + GROUPS - TAIL_GROUPS)):
             step(n)
 
-        rows_sb = short_pool.tile([P, B, 2, PACK, LT], F32, tag="raw", name="rows_sb")
-        cols_sb = short_pool.tile([P, COL_TILES, B, LT], F32, tag="raw", name="cols_sb")
+        rows_sb = keep.tile([P, B, 2, PACK, LT], F32, tag="raw_0", name="rows_sb")
+        cols_sb = keep.tile([P, COL_TILES, B, LT], F32, tag="raw_1", name="cols_sb")
 
         def copy_rows(b):
             y_sb = rows_sb[:, b, 0, :, :]

from contextlib import ExitStack

import concourse.mybir as mybir
from concourse.masks import make_identity

BF16 = mybir.dt.bfloat16
F32 = mybir.dt.float32
I32 = mybir.dt.int32
U32 = mybir.dt.uint32
U8 = mybir.dt.uint8
FP8X4 = mybir.dt.float8_e4m3fn_x4
ACT = mybir.ActivationFunctionType

P = 128
PACK = 4
K_PASS = P * PACK

B, LT, LA, DT, DA = 2, 128, 512, 1024, 7168
F = DT + DA
GROUPS = F // K_PASS
TARGET_GROUPS = DT // K_PASS
AUX_GROUPS = DA // K_PASS
N_HALF = 512
COL_TILES = (DT - N_HALF) // P

LOADS = ((0, 3), (1, 5), (0, 7), (1, 9), (0, 4))
SP_FIRST = 16
SPLIT_GROUPS = 4
TAIL_GROUPS = 5
TARGET_STEP = 8

VEC_M = 76

FLOPS = 2 * B * LT * LA * DA + 2 * B * LT * F * DT


def tile_informationfusion_pb_k_kernel(
    tc, scores, auxiliary, target, Wf_words, Wf_scales, b_f, out
):
    nc = tc.nc

    loads = []
    groups_queued = [0] * B
    for b, count in LOADS:
        loads.append((groups_queued[b], groups_queued[b] + count, b))
        groups_queued[b] += count
    assert groups_queued == [AUX_GROUPS] * B
    units = []
    first_unit = {}
    for k, (start, end, b) in enumerate(loads):
        first_unit[k] = len(units)
        for a in range(start, end):
            units.append((k, a - start, b, TARGET_GROUPS + a))
    last_load = len(loads) - 1

    with ExitStack() as ctx:
        ctx.enter_context(tc.manual_schedule())
        keep = ctx.enter_context(tc.tile_pool(name="keep", bufs=1))
        stage = ctx.enter_context(tc.tile_pool(name="stage", bufs=3))
        stage_x = ctx.enter_context(tc.tile_pool(name="stage_x", bufs=2))
        psum_y = ctx.enter_context(tc.psum_pool(name="psum_y", bufs=1))
        psum_work = ctx.enter_context(tc.psum_pool(name="psum_work", bufs=2))

        wf_planes = keep.tile([P, (GROUPS // 4) * DT], U8, align_bytes=64)
        nc.vector.memset(wf_planes[:].bitcast(I32), 0)
        bias_row = keep.tile([P, DT], BF16)
        nc.vector.memset(bias_row[:], 0.0)
        ones = keep.tile([P, 1], BF16)
        nc.vector.memset(ones[:], 1.0)
        warm = keep.tile([P, 1], F32)
        nc.vector.memset(warm[:], 0.0)
        nc.scalar.activation(out=warm[:], in_=warm[:], func=ACT.Exp)
        ident_bf = keep.tile([P, P], BF16)
        make_identity(nc, ident_bf[:])
        ident_f32 = keep.tile([P, P], F32)
        make_identity(nc, ident_f32[:])

        sc = keep.tile([P, B, LA], BF16, tag="sc_attn", align_bytes=64)
        for b in range(B):
            nc.sync.dma_start(out=sc[:, b, :], in_=scores[b])
        tg = keep.tile([P, B, DT], BF16)

        wf = [keep.tile([P, DT], U32, name="wf%d" % g, align_bytes=64) for g in range(GROUPS)]
        wf_queued = set()
        raw = {}

        def load_wf_cols(g, first, end):
            nc.sync.dma_start(
                out=wf[g][:, first:end].bitcast(I32),
                in_=Wf_words[g, :, first:end, :].rearrange("p n t -> p (n t)").bitcast(I32),
            )


        def load_wf_scales(block, quad):
            nc.sync.dma_start(
                out=wf_planes[32 * quad : 32 * quad + 16, block * DT : (block + 1) * DT].bitcast(I32),
                in_=Wf_scales[4 * block : 4 * block + 4, 4 * quad : 4 * quad + 4, :].bitcast(I32),
            )

        def load_wf(g, first, end):
            if g % 4 == 0 and g not in wf_queued:
                for quad in range(4):
                    load_wf_scales(g // 4, quad)
            wf_queued.add(g)
            load_wf_cols(g, first, end)

        def load_aux(k):
            for g in range(GROUPS):
                if g not in wf_queued and SP_FIRST + g < first_unit[k] - 1:
                    load_wf(g, 0, DT)
            start, end, b = loads[k]
            raw_k = keep.tile([P, PACK, (end - start) * K_PASS], BF16, name="raw_%d" % k, tag="raw_%d" % k)
            nc.sync.dma_start(
                out=raw_k[:],
                in_=auxiliary[b, :, start * K_PASS : end * K_PASS].rearrange(
                    "(p j) w -> p j w", j=PACK
                ),
            )
            raw[k] = raw_k
            if k == 2:
                nc.sync.dma_start(out=tg[:], in_=target.rearrange("b l d -> l b d"))
                nc.sync.dma_start(out=bias_row[0:1, :], in_=b_f.rearrange("(o n) -> o n", o=1))
            if k == last_load:
                for g in range(GROUPS - SPLIT_GROUPS):
                    if g not in wf_queued:
                        load_wf(g, 0, DT)
                for first in (0, N_HALF):
                    for g in range(GROUPS - SPLIT_GROUPS, GROUPS):
                        load_wf(g, first, first + N_HALF)

        for k in range(len(loads)):
            load_aux(k)

        grouped = {}
        aux_codes = {}
        aux_scales = {}
        banks = {}
        x_grouped = {}
        x_codes = [
            keep.tile([P, B * LT], U32, name="x_codes_%d" % g, align_bytes=64) for g in range(GROUPS)
        ]
        x_scales = [
            keep.tile([P, B * LT], U8, name="x_scales_%d" % g, align_bytes=64) for g in range(GROUPS)
        ]

        def regroup(u):
            k, place, b, g = units[u]
            grouped_u = stage.tile([P, PACK * K_PASS], BF16, tag="grouped", align_bytes=64)
            src = raw[k][:, :, place * K_PASS : (place + 1) * K_PASS].rearrange(
                "p j (m t) -> p m j t", t=PACK
            )
            dst = grouped_u[:].rearrange("p (t m j) -> p m j t", t=PACK, j=PACK)
            nc.vector.tensor_copy(out=dst[:, 0:VEC_M, :, :], in_=src[:, 0:VEC_M, :, :])
            nc.scalar.copy(out=dst[:, VEC_M:P, :, :], in_=src[:, VEC_M:P, :, :])
            grouped[u] = grouped_u

        def quantise_aux(u):
            codes = stage.tile([P, K_PASS], U32, tag="aux_codes", align_bytes=64)
            scales = stage.tile([P, K_PASS], U8, tag="aux_scales", align_bytes=64)
            nc.vector.quantize_mx(out=codes[:].bitcast(FP8X4), scales=scales[:], in_=grouped[u][:])
            aux_codes[u] = codes
            aux_scales[u] = scales

        def first_product(u):
            k, place, b, g = units[u]
            bank = psum_work.tile([P, PACK, LT], F32, tag="work")
            for t in range(PACK):
                nc.tensor.matmul_mx(
                    out=bank[:, t, :],
                    lhsT=aux_codes[u][:, t * P : (t + 1) * P].bitcast(FP8X4),
                    lhsT_scale=aux_scales[u][:, t * P : (t + 1) * P],
                    rhs=attn_codes[:, b * LT : (b + 1) * LT].bitcast(FP8X4),
                    rhs_scale=attn_scales[:, b * LT : (b + 1) * LT],
                    start=True,
                    stop=True,
                )
            banks[u] = bank

        def round_x(u):
            x_u = stage_x.tile([P, PACK * LT], BF16, tag="x_grouped", align_bytes=64)
            nc.scalar.copy(
                out=x_u[:].rearrange("p (l t) -> p l t", t=PACK),
                in_=banks[u][:].rearrange("p t l -> p l t"),
            )
            x_grouped[u] = x_u

        def quantise_x(u):
            k, place, b, g = units[u]
            nc.vector.quantize_mx(
                out=x_codes[g][:, b * LT : (b + 1) * LT].bitcast(FP8X4),
                scales=x_scales[g][:, b * LT : (b + 1) * LT],
                in_=x_grouped[u][:],
            )

        y_rows = {}
        y_cols = {}

        def second_rows(g, b):
            plane_col = (g // 4) * DT
            nc.tensor.matmul_mx(
                out=y_rows[b][:],
                lhsT=x_codes[g][:, b * LT : (b + 1) * LT].bitcast(FP8X4),
                lhsT_scale=x_scales[g][:, b * LT : (b + 1) * LT],
                rhs=wf[g][:, 0:N_HALF].bitcast(FP8X4),
                rhs_scale=wf_planes[4 * (g % 4) : P, plane_col : plane_col + N_HALF],
                start=(g == 0),
                stop=(g == GROUPS - 1),
            )

        def second_cols(g, i):
            first = N_HALF + i * P
            plane_col = (g // 4) * DT + first
            nc.tensor.matmul_mx(
                out=y_cols[i][:],
                lhsT=wf[g][:, first : first + P].bitcast(FP8X4),
                lhsT_scale=wf_planes[4 * (g % 4) : P, plane_col : plane_col + P],
                rhs=x_codes[g][:].bitcast(FP8X4),
                rhs_scale=x_scales[g][:],
                start=(g == 0),
                stop=(g == GROUPS - 1),
            )

        x_step = {}
        for u, (k, place, b, g) in enumerate(units):
            x_step[(g, b)] = u + 3

        def step(n):
            new_load = n + 1 < len(units) and units[n + 1][0] != units[n][0]
            if n + 1 < len(units) and not new_load:
                regroup(n + 1)
            if n < len(units):
                quantise_aux(n)
            if 0 <= n - 1 < len(units):
                first_product(n - 1)
            if 0 <= n - 2 < len(units):
                round_x(n - 2)
            if 0 <= n - 3 < len(units):
                quantise_x(n - 3)
            if new_load:
                regroup(n + 1)
            for g in range(GROUPS - TAIL_GROUPS):
                for b in range(B):
                    if max(SP_FIRST + g, x_step.get((g, b), 0)) == n:
                        second_rows(g, b)
                if max([SP_FIRST + g] + [x_step.get((g, b), 0) for b in range(B)]) == n:
                    for i in range(COL_TILES):
                        second_cols(g, i)

        row_max = keep.tile([P, B], F32)
        neg_max = keep.tile([P, B], F32)
        expo = keep.tile([P, B, LA], F32, tag="wide", name="expo", align_bytes=64)
        row_sum = keep.tile([P, B], F32)
        inv_sum = keep.tile([P, B], F32)
        attn = keep.tile([P, B, PACK, P], BF16)
        for b in range(B):
            nc.vector.reduce_max(
                out=row_max[:, b : b + 1], in_=sc[:, b, :], axis=mybir.AxisListType.X
            )
            nc.vector.tensor_scalar_mul(
                out=neg_max[:, b : b + 1], in0=row_max[:, b : b + 1], scalar1=-1.0
            )
            nc.scalar.activation(
                out=expo[:, b, :],
                in_=sc[:, b, :],
                func=ACT.Exp,
                bias=neg_max[:, b : b + 1],
                scale=1.0,
                accum_out=row_sum[:, b : b + 1],
            )
        for b in range(B):
            nc.vector.reciprocal(out=inv_sum[:, b : b + 1], in_=row_sum[:, b : b + 1])
            nc.vector.tensor_scalar_mul(
                out=attn[:, b, :, :],
                in0=expo[:, b, :].rearrange("l (p j) -> l j p", j=PACK),
                scalar1=inv_sum[:, b : b + 1],
            )
        regroup(0)
        step(0)
        attn_grouped = keep.tile(
            [P, B * PACK * LT], BF16, tag="sc_attn", name="attn_grouped", align_bytes=64
        )
        for b in range(B):
            attn_t = psum_work.tile([P, PACK, LT], BF16, tag="work")
            for j in range(PACK):
                nc.tensor.transpose(attn_t[:, j, :], attn[:, b, j, :], ident_bf[:])
            nc.scalar.copy(
                out=attn_grouped[:, b * PACK * LT : (b + 1) * PACK * LT].rearrange(
                    "p (l j) -> p l j", j=PACK
                ),
                in_=attn_t[:].rearrange("p j l -> p l j"),
            )
        attn_codes = keep.tile([P, B * LT], U32, align_bytes=64)
        attn_scales = keep.tile([P, B * LT], U8, align_bytes=64)
        nc.vector.quantize_mx(
            out=attn_codes[:].bitcast(FP8X4), scales=attn_scales[:], in_=attn_grouped[:]
        )
        for n in range(1, TARGET_STEP):
            step(n)

        tg_words = tg[:].bitcast(F32)
        tg_t = {}
        for b in range(B):
            tg_t[b] = psum_y.tile(
                [P, TARGET_GROUPS, 2, LT], F32, tag="y_cols_%d" % b, name="tg_t_%d" % b
            )
            for g in range(TARGET_GROUPS):
                for u in range(2):
                    nc.tensor.transpose(
                        tg_t[b][:, g, u, :],
                        tg_words[:, b, g * (K_PASS // 2) + u : (g + 1) * (K_PASS // 2) : 2],
                        ident_f32[:],
                    )
        bias_ps = psum_y.tile([P, PACK + COL_TILES], F32, tag="y_cols_2", name="bias_ps")
        for c in range(PACK):
            nc.tensor.matmul(
                out=bias_ps[:, c : c + 1],
                lhsT=bias_row[:, c:N_HALF:PACK],
                rhs=ones[:],
                start=True,
                stop=True,
            )
        for i in range(COL_TILES):
            nc.tensor.matmul(
                out=bias_ps[:, PACK + i : PACK + i + 1],
                lhsT=bias_row[:, N_HALF + i * P : N_HALF + (i + 1) * P],
                rhs=ones[:],
                start=True,
                stop=True,
            )
        step(TARGET_STEP)

        tg_grouped = keep.tile(
            [P, TARGET_GROUPS, B, LT * PACK], BF16, tag="wide", name="tg_grouped", align_bytes=64
        )
        for b in range(B):
            nc.scalar.copy(
                out=tg_grouped[:, :, b, :].bitcast(F32).rearrange("p g (l u) -> p g l u", u=2),
                in_=tg_t[b][:].rearrange("p g u l -> p g l u"),
            )
        bias_col = keep.tile([P, PACK + COL_TILES], F32)
        nc.scalar.copy(out=bias_col[:], in_=bias_ps[:])
        step(TARGET_STEP + 1)

        for g in range(TARGET_GROUPS):
            nc.vector.quantize_mx(
                out=x_codes[g][:].bitcast(FP8X4),
                scales=x_scales[g][:],
                in_=tg_grouped[:, g, :, :].rearrange("p b w -> p (b w)"),
            )
        for b in range(B):
            y_rows[b] = psum_y.tile([P, N_HALF], F32, name="y_rows_%d" % b)
        for i in range(COL_TILES):
            y_cols[i] = psum_y.tile([P, B * LT], F32, name="y_cols_%d" % i, tag="y_cols_%d" % i)

        for n in range(TARGET_STEP + 2, max(len(units) + 3, SP_FIRST + GROUPS - TAIL_GROUPS)):
            step(n)

        rows_sb = keep.tile([P, B, 2, PACK, LT], F32, tag="raw_0", name="rows_sb")
        cols_sb = keep.tile([P, COL_TILES, B, LT], F32, tag="raw_1", name="cols_sb")

        def copy_rows(b):
            y_sb = rows_sb[:, b, 0, :, :]
            nc.vector.tensor_copy(out=y_sb, in_=y_rows[b][:].rearrange("l (n c) -> l c n", c=PACK))
            return y_sb

        def finish_rows(b, y_sb):
            y_t = psum_work.tile([P, PACK, LT], F32, tag="work")
            for c in range(PACK):
                nc.tensor.transpose(y_t[:, c, :], y_sb[:, c, :], ident_f32[:])
            o_sb = rows_sb[:, b, 1, :, :]
            for c in range(PACK):
                nc.scalar.activation(
                    out=o_sb[:, c, :], in_=y_t[:, c, :], func=ACT.Tanh, bias=bias_col[:, c : c + 1], scale=1.0
                )
            nc.sync.dma_start(
                out=out[b, 0:N_HALF, :].rearrange("(n c) l -> n (c l)", c=PACK),
                in_=o_sb.rearrange("n c l -> n (c l)"),
            )

        last_groups = range(GROUPS - TAIL_GROUPS, GROUPS)
        for g in last_groups:
            for b in range(B):
                second_rows(g, b)
        y_sb = [copy_rows(b) for b in range(B)]
        for i in range(COL_TILES):
            second_cols(last_groups[0], i)
        for b in range(B):
            finish_rows(b, y_sb[b])
        for i in range(COL_TILES):
            for g in last_groups[1:]:
                second_cols(g, i)
            o_sb = cols_sb[:, i, :, :]
            nc.scalar.activation(
                out=o_sb,
                in_=y_cols[i][:].rearrange("p (b l) -> p b l", b=B),
                func=ACT.Tanh,
                bias=bias_col[:, PACK + i : PACK + i + 1],
                scale=1.0,
            )
            first = N_HALF + i * P
            nc.sync.dma_start(
                out=out[:, first : first + P, :].rearrange("b n l -> n b l"), in_=o_sb
            )
